import numpy as np
import ml_dtypes


def mxq(x, axis, fmt="e4m3"):
    dtype, down = {"e4m3": (ml_dtypes.float8_e4m3fn, 7), "e5m2": (ml_dtypes.float8_e5m2, 14)}[fmt]
    v = np.moveaxis(np.asarray(x, np.float32).astype(ml_dtypes.bfloat16).astype(np.float64), axis, -1)
    blocks = v.reshape(v.shape[:-1] + (-1, 32))
    amax = np.abs(blocks).max(-1, keepdims=True)
    byte = np.maximum(np.where(amax > 0, np.frexp(amax)[1] - 1 + 127, 0) - down, 1)
    scale = np.exp2(byte - 127.0)
    codes = (blocks / scale).astype(np.float32).astype(dtype).astype(np.float64)
    return np.moveaxis((codes * scale).reshape(v.shape), -1, axis)


WIDE = False


def mx_kscale(k):
    if not WIDE:
        return np.ones(k)
    levels = np.array([10, -10, 5, -5, 0])
    a = np.random.permutation(np.resize(levels, k // 512 * 4)).reshape(k // 512, 4)
    idx = np.arange(k)
    return np.exp2(a[idx // 512, idx % 128 // 32])


BF16 = ml_dtypes.bfloat16


def bf(x):
    return np.asarray(x, np.float32).astype(BF16)


def f64(x):
    return np.asarray(x).astype(np.float64)


B, C, PS, G, E = 64, 3, 64, 4, 256
NP = G * G
K2 = 2 * E


def setup_inputs():
    s = mx_kscale(K2)[:E]
    t = mx_kscale(K2)[:E]
    ss = np.concatenate([s, s])
    tt = np.concatenate([t, t])
    return {"tok": bf(np.random.standard_normal((B, NP, E)) * s),
            "corr_w": bf(np.random.standard_normal((E, K2)) / np.sqrt(K2) * t[:, None] / ss[None, :]),
            "corr_b": bf(np.random.standard_normal(E) * 0.3 * t),
            "cross_w": bf(np.random.standard_normal((E, K2)) / np.sqrt(K2) / tt[None, :]),
            "cross_b": bf(np.random.standard_normal(E) * 0.3)}


def reference(tok, corr_w, corr_b, cross_w, cross_b):
    xc = f64(tok)
    a = np.broadcast_to(xc[:, :, None, :], (B, NP, NP, E))
    b = np.broadcast_to(xc[:, None, :, :], (B, NP, NP, E))
    cart = np.concatenate([a, b], axis=-1)
    h = (mxq(cart, 3, "e4m3") @ mxq(f64(corr_w), 1, "e4m3").T) + f64(corr_b)
    h = h.reshape(B, NP, NP // 2, K2)
    return (mxq(h, 3, "e4m3") @ mxq(f64(cross_w), 1, "e4m3").T) + f64(cross_b)

@@ -1,0 +1,222 @@
+from contextlib import ExitStack
+
+import concourse.mybir as mybir
+from concourse.masks import make_identity
+
+F32 = mybir.dt.float32
+BF16 = mybir.dt.bfloat16
+U32 = mybir.dt.uint32
+U8 = mybir.dt.uint8
+I32 = mybir.dt.int32
+FP8X4 = mybir.dt.float8_e4m3fn_x4
+ADD = mybir.AluOpType.add
+IDENTITY = mybir.ActivationFunctionType.Identity
+
+P = 128
+PACK = 4
+HALF = 64
+B, NTOK, E = 64, 16, 256
+M_OUT = NTOK // 2
+WINDOW = 256
+N_BLOCKS = 4
+LAG = 3
+M_PER_STORE = 2
+VECTOR_EVERY = 4
+
+FLOPS = 2 * B * NTOK * NTOK * 2 * E * E + 2 * B * NTOK * M_OUT * 2 * E * E
+
+
+def tile_simplemodel_pb_t_kernel(tc, tok, corr_w, corr_b, cross_w, cross_b, out):
+    nc = tc.nc
+    with ExitStack() as ctx:
+        const = ctx.enter_context(tc.tile_pool(name="const", bufs=1))
+        g_pool = ctx.enter_context(tc.tile_pool(name="g", bufs=LAG + 2))
+        out_pool = ctx.enter_context(tc.tile_pool(name="rows", bufs=4))
+        psum_h = ctx.enter_context(tc.psum_pool(name="psum_h", bufs=6))
+        psum_o = ctx.enter_context(tc.psum_pool(name="psum_o", bufs=2))
+
+        tok_sb = const.tile([P, 8 * E], BF16)
+        nc.sync.dma_start(out=tok_sb[:], in_=tok.rearrange("b (x r) k -> (b x) (r k)", x=2))
+        cw_sb = const.tile([P, 2, 2, 2 * E], BF16)
+        cw_rows = corr_w.rearrange("(h p) k -> p h k", p=P)
+        nc.scalar.dma_start(out=cw_sb[:, 0, :, :], in_=cw_rows)
+        nc.scalar.dma_start(out=cw_sb[:, 1, :, 0:E], in_=cw_rows[:, :, E : 2 * E])
+        nc.scalar.dma_start(out=cw_sb[:, 1, :, E : 2 * E], in_=cw_rows[:, :, 0:E])
+        xw_sb = const.tile([P, 2, 2 * E], BF16)
+        nc.scalar.dma_start(out=xw_sb[:], in_=cross_w.rearrange("(h p) k -> p h k", p=P))
+        cb_rows = const.tile([P, P], BF16)
+        nc.vector.memset(cb_rows[:], 0.0)
+        nc.gpsimd.dma_start(out=cb_rows[0:2, :], in_=corr_b.rearrange("(h e) -> h e", h=2))
+        xb_bf = const.tile([P, E], BF16)
+        nc.gpsimd.dma_start(out=xb_bf[:], in_=cross_b.partition_broadcast(P))
+
+        ident_f32 = const.tile([P, P], F32)
+        make_identity(nc, ident_f32[:])
+        ident_bf = const.tile([P, P], BF16)
+        make_identity(nc, ident_bf[:])
+
+        w1_grouped = const.tile([P, 8 * P * PACK], BF16, align_bytes=64)
+        nc.vector.memset(w1_grouped[:].bitcast(I32), 0)
+        w1_words = w1_grouped[:].bitcast(F32).rearrange("p (v e u) -> p v e u", v=8, u=2)
+        cw_words = cw_sb[:].rearrange("p s h k -> p (s h k)").bitcast(F32).rearrange("p (v q u) -> p v u q", v=4, u=2)
+        for s in range(2):
+            wt = psum_h.tile([P, 2, 2, P], F32, tag="h")
+            for eh in range(2):
+                for u in range(2):
+                    nc.tensor.transpose(wt[:, eh, u, :], cw_words[:, 2 * s + eh, u, :], ident_f32[:])
+            for half in range(2):
+                kind = half if s == 0 else 1 - half
+                v = 4 * kind + 2 * half
+                rows = slice(HALF * half, HALF * (half + 1))
+                src = wt[rows].rearrange("p h u e -> p h e u")
+                if s == 0:
+                    nc.scalar.copy(out=w1_words[rows, v : v + 2, :, :], in_=src)
+                else:
+                    nc.vector.tensor_copy(out=w1_words[rows, v : v + 2, :, :], in_=src)
+        w1_codes = const.tile([P, 8 * P], U32, align_bytes=64)
+        w1_scales = const.tile([P, 8 * P], U8, align_bytes=64)
+        nc.vector.quantize_mx(out=w1_codes[:].bitcast(FP8X4), scales=w1_scales[:], in_=w1_grouped[:])
+
+        tok_words = tok_sb[:].bitcast(F32).rearrange("p (n q u) -> p n u q", n=N_BLOCKS, u=2)
+        xts = []
+        for pair in range(2):
+            xt = psum_h.tile([P, 2, 2, P], F32, tag="h", name="xt%d" % pair)
+            for nb in range(2):
+                for u in range(2):
+                    nc.tensor.transpose(xt[:, nb, u, :], tok_words[:, 2 * pair + nb, u, :], ident_f32[:])
+            xts.append(xt)
+        i_grouped = const.tile([P, N_BLOCKS * P * PACK], BF16, align_bytes=64)
+        i_words = i_grouped[:].bitcast(F32).rearrange("p (n c u) -> p n c u", n=N_BLOCKS, u=2)
+        for pair in range(2):
+            nc.scalar.copy(
+                out=i_words[:, 2 * pair : 2 * pair + 2, :, :],
+                in_=xts[pair][:].rearrange("p n u c -> p n c u"),
+            )
+        i_codes = const.tile([P, N_BLOCKS * P], U32, align_bytes=64)
+        i_scales = const.tile([P, N_BLOCKS * P], U8, align_bytes=64)
+        nc.vector.quantize_mx(out=i_codes[:].bitcast(FP8X4), scales=i_scales[:], in_=i_grouped[:])
+
+        j_grouped = const.tile([P, M_OUT * WINDOW * PACK], BF16, align_bytes=64)
+        j_words = j_grouped[:].bitcast(F32).rearrange(
+            "p (m l b d u) -> p m l b d u", m=M_OUT, l=2, d=2, u=2
+        )
+        j_codes = const.tile([P, M_OUT * WINDOW], U32, align_bytes=64)
+        j_scales = const.tile([P, M_OUT * WINDOW], U8, align_bytes=64)
+        for m in range(M_OUT):
+            n, x = m % N_BLOCKS, m // N_BLOCKS
+            src = xts[n // 2][:, n % 2, :, :].rearrange("p u (b x) -> p x b u", x=2)[:, x, :, :]
+            src = src.unsqueeze(2).to_broadcast([P, B, 2, 2])
+            nc.scalar.copy(out=j_words[:, m, 0, :, :, :], in_=src)
+            nc.vector.tensor_copy(out=j_words[:, m, 1, :, :, :], in_=src)
+            cols = slice(m * WINDOW, (m + 1) * WINDOW)
+            nc.vector.quantize_mx(
+                out=j_codes[:, cols].bitcast(FP8X4),
+                scales=j_scales[:, cols],
+                in_=j_grouped[:, m * WINDOW * PACK : (m + 1) * WINDOW * PACK],
+            )
+
+        wct = psum_h.tile([P, PACK, E], BF16, tag="h")
+        for eh in range(2):
+            for par in range(2):
+                for hh in range(2):
+                    first = E * par + P * eh
+                    nc.tensor.transpose(
+                        wct[:, 2 * eh + par, hh * P : (hh + 1) * P], xw_sb[:, hh, first : first + P], ident_bf[:]
+                    )
+        cbt = psum_h.tile([P, P], BF16, tag="h")
+        nc.tensor.transpose(cbt[:], cb_rows[:], ident_bf[:])
+        w2_grouped = const.tile([P, E, PACK], BF16, align_bytes=64)
+        nc.scalar.copy(out=w2_grouped[:], in_=wct[:].rearrange("p t e -> p e t"))
+        w2_codes = const.tile([P, E], U32, align_bytes=64)
+        w2_scales = const.tile([P, E], U8, align_bytes=64)
+        nc.vector.quantize_mx(
+            out=w2_codes[:].bitcast(FP8X4), scales=w2_scales[:], in_=w2_grouped[:].rearrange("p e t -> p (e t)")
+        )
+        corr_bias = const.tile([P, 2], F32)
+        nc.vector.tensor_copy(out=corr_bias[:], in_=cbt[:, 0:2])
+        cross_bias = const.tile([P, E], F32)
+        nc.vector.tensor_copy(out=cross_bias[:], in_=xb_bf[:])
+
+        out_rows = out.rearrange("b (x n a) m e -> (b x) n a (m e)", x=2, n=N_BLOCKS, a=2)
+
+        units = [(a, n0, m) for a in range(2) for n0 in range(0, N_BLOCKS, 2) for m in range(M_OUT)]
+        g_codes = {}
+        g_scales = {}
+        stores = {}
+
+        def first_stage(k):
+            a, n0, m = units[k]
+            g_grouped = g_pool.tile([P, WINDOW, 2, 2], BF16, align_bytes=64, tag="g_grouped", name="g_grouped")
+            for eh in range(2):
+                h_ps = psum_h.tile([P, 2, WINDOW], F32, tag="h", name="h_ps")
+                for par in range(2):
+                    va = (2 * a + eh) * P
+                    vb = (4 + 2 * par + eh) * P
+                    nc.tensor.matmul_mx(
+                        out=h_ps[:, par, :],
+                        lhsT=w1_codes[:, va : va + P].bitcast(FP8X4),
+                        lhsT_scale=w1_scales[:, va : va + P],
+                        rhs=i_codes[:, n0 * P : n0 * P + WINDOW].bitcast(FP8X4),
+                        rhs_scale=i_scales[:, n0 * P : n0 * P + WINDOW],
+                        start=True,
+                        stop=False,
+                    )
+                    nc.tensor.matmul_mx(
+                        out=h_ps[:, par, :],
+                        lhsT=w1_codes[:, vb : vb + P].bitcast(FP8X4),
+                        lhsT_scale=w1_scales[:, vb : vb + P],
+                        rhs=j_codes[:, m * WINDOW : (m + 1) * WINDOW].bitcast(FP8X4),
+                        rhs_scale=j_scales[:, m * WINDOW : (m + 1) * WINDOW],
+                        start=False,
+                        stop=True,
+                    )
+                src = h_ps[:].rearrange("p g c -> p c g")
+                if k % VECTOR_EVERY == VECTOR_EVERY - 1:
+                    nc.vector.tensor_scalar_add(out=g_grouped[:, :, eh, :], in0=src, scalar1=corr_bias[:, eh : eh + 1])
+                else:
+                    nc.scalar.activation(
+                        out=g_grouped[:, :, eh, :], in_=src, func=IDENTITY, bias=corr_bias[:, eh : eh + 1], scale=1.0
+                    )
+            codes = g_pool.tile([P, WINDOW], U32, align_bytes=64, tag="g_codes", name="codes")
+            scales = g_pool.tile([P, WINDOW], U8, align_bytes=64, tag="g_scales", name="scales")
+            nc.vector.quantize_mx(
+                out=codes[:].bitcast(FP8X4), scales=scales[:], in_=g_grouped[:].rearrange("p c h g -> p (c h g)")
+            )
+            g_codes[k] = codes
+            g_scales[k] = scales
+
+        def second_stage(k):
+            a, n0, m = units[k]
+            o_ps = psum_o.tile([P, 2, E], F32, tag="o", name="o_ps")
+            for l in range(2):
+                nc.tensor.matmul_mx(
+                    out=o_ps[:, l, :],
+                    lhsT=g_codes[k][:, l * P : (l + 1) * P].bitcast(FP8X4),
+                    lhsT_scale=g_scales[k][:, l * P : (l + 1) * P],
+                    rhs=w2_codes[:].bitcast(FP8X4),
+                    rhs_scale=w2_scales[:],
+                    start=True,
+                    stop=True,
+                )
+            if m % M_PER_STORE == 0:
+                rows = out_pool.tile([P, 2, M_PER_STORE, E], F32, tag="rows", name="rows")
+                stores[0] = rows
+            rows = stores[0]
+            nc.vector.tensor_tensor(
+                out=rows[:, :, m % M_PER_STORE, :],
+                in0=o_ps[:],
+                in1=cross_bias[:].unsqueeze(1).to_broadcast([P, 2, E]),
+                op=ADD,
+            )
+            if m % M_PER_STORE == M_PER_STORE - 1:
+                first = (m + 1 - M_PER_STORE) * E
+                nc.sync.dma_start(
+                    out=out_rows[:, n0 : n0 + 2, a, first : first + M_PER_STORE * E],
+                    in_=rows[:].rearrange("p l m e -> p l (m e)"),
+                )
+
+        for step in range(len(units) + LAG):
+            if step < len(units):
+                first_stage(step)
+            if step >= LAG:
+                second_stage(step - LAG)

@@ -17,9 +17,8 @@ PACK = 4
 HALF = 64
 B, NTOK, E = 64, 16, 256
 M_OUT = NTOK // 2
-WINDOW = 256
 N_BLOCKS = 4
-LAG = 3
+WINDOW = 2 * P
 M_PER_STORE = 2
 VECTOR_EVERY = 4
 
@@ -30,11 +29,15 @@ def tile_simplemodel_pb_t_kernel(tc, tok, corr_w, corr_b, cross_w, cross_b, out)
     nc = tc.nc
     with ExitStack() as ctx:
         const = ctx.enter_context(tc.tile_pool(name="const", bufs=1))
-        g_pool = ctx.enter_context(tc.tile_pool(name="g", bufs=LAG + 2))
+        g_pool = ctx.enter_context(tc.tile_pool(name="g", bufs=4))
         out_pool = ctx.enter_context(tc.tile_pool(name="rows", bufs=4))
         psum_h = ctx.enter_context(tc.psum_pool(name="psum_h", bufs=6))
         psum_o = ctx.enter_context(tc.psum_pool(name="psum_o", bufs=2))
 
+        ident_f32 = const.tile([P, P], F32)
+        make_identity(nc, ident_f32[:])
+        ident_bf = const.tile([P, P], BF16)
+        nc.vector.tensor_copy(out=ident_bf[:], in_=ident_f32[:])
         tok_sb = const.tile([P, 8 * E], BF16)
         nc.sync.dma_start(out=tok_sb[:], in_=tok.rearrange("b (x r) k -> (b x) (r k)", x=2))
         cw_sb = const.tile([P, 2, 2, 2 * E], BF16)
@@ -42,18 +45,13 @@ def tile_simplemodel_pb_t_kernel(tc, tok, corr_w, corr_b, cross_w, cross_b, out)
         nc.scalar.dma_start(out=cw_sb[:, 0, :, :], in_=cw_rows)
         nc.scalar.dma_start(out=cw_sb[:, 1, :, 0:E], in_=cw_rows[:, :, E : 2 * E])
         nc.scalar.dma_start(out=cw_sb[:, 1, :, E : 2 * E], in_=cw_rows[:, :, 0:E])
-        xw_sb = const.tile([P, 2, 2 * E], BF16)
-        nc.scalar.dma_start(out=xw_sb[:], in_=cross_w.rearrange("(h p) k -> p h k", p=P))
         cb_rows = const.tile([P, P], BF16)
         nc.vector.memset(cb_rows[:], 0.0)
-        nc.gpsimd.dma_start(out=cb_rows[0:2, :], in_=corr_b.rearrange("(h e) -> h e", h=2))
+        nc.sync.dma_start(out=cb_rows[0:2, :], in_=corr_b.rearrange("(h e) -> h e", h=2))
+        xw_sb = const.tile([P, 2, 2 * E], BF16)
+        nc.scalar.dma_start(out=xw_sb[:], in_=cross_w.rearrange("(h p) k -> p h k", p=P))
         xb_bf = const.tile([P, E], BF16)
         nc.gpsimd.dma_start(out=xb_bf[:], in_=cross_b.partition_broadcast(P))
-
-        ident_f32 = const.tile([P, P], F32)
-        make_identity(nc, ident_f32[:])
-        ident_bf = const.tile([P, P], BF16)
-        make_identity(nc, ident_bf[:])
 
         w1_grouped = const.tile([P, 8 * P * PACK], BF16, align_bytes=64)
         nc.vector.memset(w1_grouped[:].bitcast(I32), 0)
@@ -77,6 +75,10 @@ def tile_simplemodel_pb_t_kernel(tc, tok, corr_w, corr_b, cross_w, cross_b, out)
         w1_scales = const.tile([P, 8 * P], U8, align_bytes=64)
         nc.vector.quantize_mx(out=w1_codes[:].bitcast(FP8X4), scales=w1_scales[:], in_=w1_grouped[:])
 
+        def w1(kind, half, eh):
+            v = 4 * kind + 2 * half + eh
+            return w1_codes[:, v * P : (v + 1) * P].bitcast(FP8X4), w1_scales[:, v * P : (v + 1) * P]
+
         tok_words = tok_sb[:].bitcast(F32).rearrange("p (n q u) -> p n u q", n=N_BLOCKS, u=2)
         xts = []
         for pair in range(2):
@@ -85,21 +87,31 @@ def tile_simplemodel_pb_t_kernel(tc, tok, corr_w, corr_b, cross_w, cross_b, out)
                 for u in range(2):
                     nc.tensor.transpose(xt[:, nb, u, :], tok_words[:, 2 * pair + nb, u, :], ident_f32[:])
             xts.append(xt)
+        wct = psum_h.tile([P, PACK, E], BF16, tag="h")
+        for eh in range(2):
+            for par in range(2):
+                for hh in range(2):
+                    first = E * par + P * eh
+                    nc.tensor.transpose(
+                        wct[:, 2 * eh + par, hh * P : (hh + 1) * P], xw_sb[:, hh, first : first + P], ident_bf[:]
+                    )
+        cbt = psum_h.tile([P, P], BF16, tag="h")
+        nc.tensor.transpose(cbt[:], cb_rows[:], ident_bf[:])
+        corr_bias = const.tile([P, 2], F32)
+        nc.vector.tensor_copy(out=corr_bias[:], in_=cbt[:, 0:2])
+
         i_grouped = const.tile([P, N_BLOCKS * P * PACK], BF16, align_bytes=64)
         i_words = i_grouped[:].bitcast(F32).rearrange("p (n c u) -> p n c u", n=N_BLOCKS, u=2)
         for pair in range(2):
             nc.scalar.copy(
-                out=i_words[:, 2 * pair : 2 * pair + 2, :, :],
-                in_=xts[pair][:].rearrange("p n u c -> p n c u"),
+                out=i_words[:, 2 * pair : 2 * pair + 2, :, :], in_=xts[pair][:].rearrange("p n u c -> p n c u")
             )
         i_codes = const.tile([P, N_BLOCKS * P], U32, align_bytes=64)
         i_scales = const.tile([P, N_BLOCKS * P], U8, align_bytes=64)
         nc.vector.quantize_mx(out=i_codes[:].bitcast(FP8X4), scales=i_scales[:], in_=i_grouped[:])
 
         j_grouped = const.tile([P, M_OUT * WINDOW * PACK], BF16, align_bytes=64)
-        j_words = j_grouped[:].bitcast(F32).rearrange(
-            "p (m l b d u) -> p m l b d u", m=M_OUT, l=2, d=2, u=2
-        )
+        j_words = j_grouped[:].bitcast(F32).rearrange("p (m l b d u) -> p m l b d u", m=M_OUT, l=2, d=2, u=2)
         j_codes = const.tile([P, M_OUT * WINDOW], U32, align_bytes=64)
         j_scales = const.tile([P, M_OUT * WINDOW], U8, align_bytes=64)
         for m in range(M_OUT):
@@ -115,16 +127,19 @@ def tile_simplemodel_pb_t_kernel(tc, tok, corr_w, corr_b, cross_w, cross_b, out)
                 in_=j_grouped[:, m * WINDOW * PACK : (m + 1) * WINDOW * PACK],
             )
 
-        wct = psum_h.tile([P, PACK, E], BF16, tag="h")
-        for eh in range(2):
-            for par in range(2):
-                for hh in range(2):
-                    first = E * par + P * eh
-                    nc.tensor.transpose(
-                        wct[:, 2 * eh + par, hh * P : (hh + 1) * P], xw_sb[:, hh, first : first + P], ident_bf[:]
-                    )
-        cbt = psum_h.tile([P, P], BF16, tag="h")
-        nc.tensor.transpose(cbt[:], cb_rows[:], ident_bf[:])
+        a_term = const.tile([P, 2, 2, N_BLOCKS * P], F32)
+        for a in range(2):
+            for eh in range(2):
+                a_ps = psum_h.tile([P, N_BLOCKS * P], F32, tag="h", name="a_ps")
+                codes, scales = w1(0, a, eh)
+                nc.tensor.matmul_mx(
+                    out=a_ps[:], lhsT=codes, lhsT_scale=scales, rhs=i_codes[:].bitcast(FP8X4), rhs_scale=i_scales[:],
+                    start=True, stop=True,
+                )
+                nc.scalar.activation(
+                    out=a_term[:, a, eh, :], in_=a_ps[:], func=IDENTITY, bias=corr_bias[:, eh : eh + 1], scale=1.0
+                )
+
         w2_grouped = const.tile([P, E, PACK], BF16, align_bytes=64)
         nc.scalar.copy(out=w2_grouped[:], in_=wct[:].rearrange("p t e -> p e t"))
         w2_codes = const.tile([P, E], U32, align_bytes=64)
@@ -132,81 +147,95 @@ def tile_simplemodel_pb_t_kernel(tc, tok, corr_w, corr_b, cross_w, cross_b, out)
         nc.vector.quantize_mx(
             out=w2_codes[:].bitcast(FP8X4), scales=w2_scales[:], in_=w2_grouped[:].rearrange("p e t -> p (e t)")
         )
-        corr_bias = const.tile([P, 2], F32)
-        nc.vector.tensor_copy(out=corr_bias[:], in_=cbt[:, 0:2])
         cross_bias = const.tile([P, E], F32)
         nc.vector.tensor_copy(out=cross_bias[:], in_=xb_bf[:])
 
         out_rows = out.rearrange("b (x n a) m e -> (b x) n a (m e)", x=2, n=N_BLOCKS, a=2)
 
         units = [(a, n0, m) for a in range(2) for n0 in range(0, N_BLOCKS, 2) for m in range(M_OUT)]
-        g_codes = {}
-        g_scales = {}
-        stores = {}
+        grouped_of = {}
+        codes_of = {}
+        banks_of = {}
+        rows_of = {}
 
-        def first_stage(k):
+        def by_vector(k):
+            return k % VECTOR_EVERY == VECTOR_EVERY - 1
+
+        def make_h(k):
             a, n0, m = units[k]
             g_grouped = g_pool.tile([P, WINDOW, 2, 2], BF16, align_bytes=64, tag="g_grouped", name="g_grouped")
-            for eh in range(2):
-                h_ps = psum_h.tile([P, 2, WINDOW], F32, tag="h", name="h_ps")
-                for par in range(2):
-                    va = (2 * a + eh) * P
-                    vb = (4 + 2 * par + eh) * P
-                    nc.tensor.matmul_mx(
-                        out=h_ps[:, par, :],
-                        lhsT=w1_codes[:, va : va + P].bitcast(FP8X4),
-                        lhsT_scale=w1_scales[:, va : va + P],
-                        rhs=i_codes[:, n0 * P : n0 * P + WINDOW].bitcast(FP8X4),
-                        rhs_scale=i_scales[:, n0 * P : n0 * P + WINDOW],
-                        start=True,
-                        stop=False,
+            grouped_of[k] = g_grouped
+            j_cols = slice(m * WINDOW, (m + 1) * WINDOW)
+            if by_vector(k):
+                b_ps = psum_h.tile([P, 2, 2, P], F32, tag="h", name="b_ps")
+                for eh in range(2):
+                    for par in range(2):
+                        codes, scales = w1(1, par, eh)
+                        nc.tensor.matmul_mx(
+                            out=b_ps[:, eh, par, :], lhsT=codes, lhsT_scale=scales,
+                            rhs=j_codes[:, m * WINDOW : m * WINDOW + P].bitcast(FP8X4),
+                            rhs_scale=j_scales[:, m * WINDOW : m * WINDOW + P],
+                            start=True, stop=True,
+                        )
+                for l in range(2):
+                    n = n0 + l
+                    stored = a_term[:, a, :, n * P : (n + 1) * P].rearrange("p h c -> p c h")
+                    nc.vector.tensor_tensor(
+                        out=g_grouped[:, l * P : (l + 1) * P, :, :],
+                        in0=b_ps[:].rearrange("p h g c -> p c h g"),
+                        in1=stored.unsqueeze(3).to_broadcast([P, P, 2, 2]),
+                        op=ADD,
                     )
-                    nc.tensor.matmul_mx(
-                        out=h_ps[:, par, :],
-                        lhsT=w1_codes[:, vb : vb + P].bitcast(FP8X4),
-                        lhsT_scale=w1_scales[:, vb : vb + P],
-                        rhs=j_codes[:, m * WINDOW : (m + 1) * WINDOW].bitcast(FP8X4),
-                        rhs_scale=j_scales[:, m * WINDOW : (m + 1) * WINDOW],
-                        start=False,
-                        stop=True,
-                    )
-                src = h_ps[:].rearrange("p g c -> p c g")
-                if k % VECTOR_EVERY == VECTOR_EVERY - 1:
-                    nc.vector.tensor_scalar_add(out=g_grouped[:, :, eh, :], in0=src, scalar1=corr_bias[:, eh : eh + 1])
-                else:
+            else:
+                for eh in range(2):
+                    h_ps = psum_h.tile([P, 2, WINDOW], F32, tag="h", name="h_ps")
+                    for par in range(2):
+                        codes, scales = w1(0, a, eh)
+                        nc.tensor.matmul_mx(
+                            out=h_ps[:, par, :], lhsT=codes, lhsT_scale=scales,
+                            rhs=i_codes[:, n0 * P : n0 * P + WINDOW].bitcast(FP8X4),
+                            rhs_scale=i_scales[:, n0 * P : n0 * P + WINDOW],
+                            start=True, stop=False,
+                        )
+                        codes, scales = w1(1, par, eh)
+                        nc.tensor.matmul_mx(
+                            out=h_ps[:, par, :], lhsT=codes, lhsT_scale=scales,
+                            rhs=j_codes[:, j_cols].bitcast(FP8X4), rhs_scale=j_scales[:, j_cols],
+                            start=False, stop=True,
+                        )
                     nc.scalar.activation(
-                        out=g_grouped[:, :, eh, :], in_=src, func=IDENTITY, bias=corr_bias[:, eh : eh + 1], scale=1.0
+                        out=g_grouped[:, :, eh, :], in_=h_ps[:].rearrange("p g c -> p c g"),
+                        func=IDENTITY, bias=corr_bias[:, eh : eh + 1], scale=1.0,
                     )
+
+        def quantise_g(k):
             codes = g_pool.tile([P, WINDOW], U32, align_bytes=64, tag="g_codes", name="codes")
             scales = g_pool.tile([P, WINDOW], U8, align_bytes=64, tag="g_scales", name="scales")
             nc.vector.quantize_mx(
-                out=codes[:].bitcast(FP8X4), scales=scales[:], in_=g_grouped[:].rearrange("p c h g -> p (c h g)")
+                out=codes[:].bitcast(FP8X4), scales=scales[:], in_=grouped_of[k][:].rearrange("p c h g -> p (c h g)")
             )
-            g_codes[k] = codes
-            g_scales[k] = scales
+            codes_of[k] = (codes, scales)
 
-        def second_stage(k):
-            a, n0, m = units[k]
+        def second_matmul(k):
+            codes, scales = codes_of[k]
             o_ps = psum_o.tile([P, 2, E], F32, tag="o", name="o_ps")
             for l in range(2):
                 nc.tensor.matmul_mx(
                     out=o_ps[:, l, :],
-                    lhsT=g_codes[k][:, l * P : (l + 1) * P].bitcast(FP8X4),
-                    lhsT_scale=g_scales[k][:, l * P : (l + 1) * P],
-                    rhs=w2_codes[:].bitcast(FP8X4),
-                    rhs_scale=w2_scales[:],
-                    start=True,
-                    stop=True,
+                    lhsT=codes[:, l * P : (l + 1) * P].bitcast(FP8X4), lhsT_scale=scales[:, l * P : (l + 1) * P],
+                    rhs=w2_codes[:].bitcast(FP8X4), rhs_scale=w2_scales[:],
+                    start=True, stop=True,
                 )
+            banks_of[k] = o_ps
+
+        def bias_and_store(k):
+            a, n0, m = units[k]
             if m % M_PER_STORE == 0:
-                rows = out_pool.tile([P, 2, M_PER_STORE, E], F32, tag="rows", name="rows")
-                stores[0] = rows
-            rows = stores[0]
+                rows_of[0] = out_pool.tile([P, 2, M_PER_STORE, E], F32, tag="rows", name="rows")
+            rows = rows_of[0]
             nc.vector.tensor_tensor(
-                out=rows[:, :, m % M_PER_STORE, :],
-                in0=o_ps[:],
-                in1=cross_bias[:].unsqueeze(1).to_broadcast([P, 2, E]),
-                op=ADD,
+                out=rows[:, :, m % M_PER_STORE, :], in0=banks_of[k][:],
+                in1=cross_bias[:].unsqueeze(1).to_broadcast([P, 2, E]), op=ADD,
             )
             if m % M_PER_STORE == M_PER_STORE - 1:
                 first = (m + 1 - M_PER_STORE) * E
@@ -215,8 +244,14 @@ def tile_simplemodel_pb_t_kernel(tc, tok, corr_w, corr_b, cross_w, cross_b, out)
                     in_=rows[:].rearrange("p l m e -> p l (m e)"),
                 )
 
-        for step in range(len(units) + LAG):
-            if step < len(units):
-                first_stage(step)
-            if step >= LAG:
-                second_stage(step - LAG)
+        n_units = len(units)
+        with tc.manual_schedule():
+            for step in range(n_units + 4):
+                if 0 <= step - 4:
+                    bias_and_store(step - 4)
+                if step < n_units:
+                    make_h(step)
+                if 0 <= step - 2 < n_units:
+                    quantise_g(step - 2)
+                if 0 <= step - 3 < n_units:
+                    second_matmul(step - 3)

@@ -20,7 +20,7 @@ M_OUT = NTOK // 2
 N_BLOCKS = 4
 WINDOW = 2 * P
 M_PER_STORE = 2
-VECTOR_EVERY = 4
+VECTOR_EVERY = 2
 
 FLOPS = 2 * B * NTOK * NTOK * 2 * E * E + 2 * B * NTOK * M_OUT * 2 * E * E
 
@@ -29,7 +29,7 @@ def tile_simplemodel_pb_t_kernel(tc, tok, corr_w, corr_b, cross_w, cross_b, out)
     nc = tc.nc
     with ExitStack() as ctx:
         const = ctx.enter_context(tc.tile_pool(name="const", bufs=1))
-        g_pool = ctx.enter_context(tc.tile_pool(name="g", bufs=4))
+        g_pool = ctx.enter_context(tc.tile_pool(name="g", bufs=6))
         out_pool = ctx.enter_context(tc.tile_pool(name="rows", bufs=4))
         psum_h = ctx.enter_context(tc.psum_pool(name="psum_h", bufs=6))
         psum_o = ctx.enter_context(tc.psum_pool(name="psum_o", bufs=2))
@@ -246,12 +246,12 @@ def tile_simplemodel_pb_t_kernel(tc, tok, corr_w, corr_b, cross_w, cross_b, out)
 
         n_units = len(units)
         with tc.manual_schedule():
-            for step in range(n_units + 4):
-                if 0 <= step - 4:
-                    bias_and_store(step - 4)
+            for step in range(n_units + 5):
+                if 0 <= step - 5:
+                    bias_and_store(step - 5)
                 if step < n_units:
                     make_h(step)
-                if 0 <= step - 2 < n_units:
-                    quantise_g(step - 2)
                 if 0 <= step - 3 < n_units:
-                    second_matmul(step - 3)
+                    quantise_g(step - 3)
+                if 0 <= step - 4 < n_units:
+                    second_matmul(step - 4)

@@ -20,7 +20,8 @@ M_OUT = NTOK // 2
 N_BLOCKS = 4
 WINDOW = 2 * P
 M_PER_STORE = 2
-VECTOR_EVERY = 2
+TURNS = 5
+VECTOR_TURNS = (1, 3)
 
 FLOPS = 2 * B * NTOK * NTOK * 2 * E * E + 2 * B * NTOK * M_OUT * 2 * E * E
 
@@ -39,19 +40,22 @@ def tile_simplemodel_pb_t_kernel(tc, tok, corr_w, corr_b, cross_w, cross_b, out)
         ident_bf = const.tile([P, P], BF16)
         nc.vector.tensor_copy(out=ident_bf[:], in_=ident_f32[:])
         tok_sb = const.tile([P, 8 * E], BF16)
-        nc.sync.dma_start(out=tok_sb[:], in_=tok.rearrange("b (x r) k -> (b x) (r k)", x=2))
+        tok_rows = tok.rearrange("b (x r) k -> (b x) (r k)", x=2)
+        nc.sync.dma_start(out=tok_sb[:, 0 : 4 * E], in_=tok_rows[:, 0 : 4 * E])
+        nc.sync.dma_start(out=tok_sb[:, 4 * E : 8 * E], in_=tok_rows[:, 4 * E : 8 * E])
         cw_sb = const.tile([P, 2, 2, 2 * E], BF16)
         cw_rows = corr_w.rearrange("(h p) k -> p h k", p=P)
         nc.scalar.dma_start(out=cw_sb[:, 0, :, :], in_=cw_rows)
         nc.scalar.dma_start(out=cw_sb[:, 1, :, 0:E], in_=cw_rows[:, :, E : 2 * E])
         nc.scalar.dma_start(out=cw_sb[:, 1, :, E : 2 * E], in_=cw_rows[:, :, 0:E])
-        cb_rows = const.tile([P, P], BF16)
-        nc.vector.memset(cb_rows[:], 0.0)
-        nc.sync.dma_start(out=cb_rows[0:2, :], in_=corr_b.rearrange("(h e) -> h e", h=2))
+        bias_rows = const.tile([P, P + E], BF16)
+        nc.vector.memset(bias_rows[:], 0.0)
+        nc.sync.dma_start(out=bias_rows[0:2, 0:P], in_=corr_b.rearrange("(h e) -> h e", h=2))
+        nc.sync.dma_start(out=bias_rows[0:1, P : P + E], in_=cross_b.rearrange("(o e) -> o e", o=1))
+        ones = const.tile([P, P], BF16)
+        nc.vector.memset(ones[:], 1.0)
         xw_sb = const.tile([P, 2, 2 * E], BF16)
         nc.scalar.dma_start(out=xw_sb[:], in_=cross_w.rearrange("(h p) k -> p h k", p=P))
-        xb_bf = const.tile([P, E], BF16)
-        nc.gpsimd.dma_start(out=xb_bf[:], in_=cross_b.partition_broadcast(P))
 
         w1_grouped = const.tile([P, 8 * P * PACK], BF16, align_bytes=64)
         nc.vector.memset(w1_grouped[:].bitcast(I32), 0)
@@ -96,7 +100,9 @@ def tile_simplemodel_pb_t_kernel(tc, tok, corr_w, corr_b, cross_w, cross_b, out)
                         wct[:, 2 * eh + par, hh * P : (hh + 1) * P], xw_sb[:, hh, first : first + P], ident_bf[:]
                     )
         cbt = psum_h.tile([P, P], BF16, tag="h")
-        nc.tensor.transpose(cbt[:], cb_rows[:], ident_bf[:])
+        nc.tensor.transpose(cbt[:], bias_rows[:, 0:P], ident_bf[:])
+        xb_ps = psum_h.tile([P, E], F32, tag="h")
+        nc.tensor.matmul(out=xb_ps[:], lhsT=ones[:], rhs=bias_rows[:, P : P + E], start=True, stop=True)
         corr_bias = const.tile([P, 2], F32)
         nc.vector.tensor_copy(out=corr_bias[:], in_=cbt[:, 0:2])
 
@@ -148,7 +154,7 @@ def tile_simplemodel_pb_t_kernel(tc, tok, corr_w, corr_b, cross_w, cross_b, out)
             out=w2_codes[:].bitcast(FP8X4), scales=w2_scales[:], in_=w2_grouped[:].rearrange("p e t -> p (e t)")
         )
         cross_bias = const.tile([P, E], F32)
-        nc.vector.tensor_copy(out=cross_bias[:], in_=xb_bf[:])
+        nc.scalar.copy(out=cross_bias[:], in_=xb_ps[:])
 
         out_rows = out.rearrange("b (x n a) m e -> (b x) n a (m e)", x=2, n=N_BLOCKS, a=2)
 
@@ -159,7 +165,7 @@ def tile_simplemodel_pb_t_kernel(tc, tok, corr_w, corr_b, cross_w, cross_b, out)
         rows_of = {}
 
         def by_vector(k):
-            return k % VECTOR_EVERY == VECTOR_EVERY - 1
+            return k % TURNS in VECTOR_TURNS
 
         def make_h(k):
             a, n0, m = units[k]

@@ -20,14 +20,15 @@ M_OUT = NTOK // 2
 N_BLOCKS = 4
 WINDOW = 2 * P
 M_PER_STORE = 2
-TURNS = 5
-VECTOR_TURNS = (1, 3)
+ROUTE = "SSGSSGSG"
+PAIR = 2
 
 FLOPS = 2 * B * NTOK * NTOK * 2 * E * E + 2 * B * NTOK * M_OUT * 2 * E * E
 
 
 def tile_simplemodel_pb_t_kernel(tc, tok, corr_w, corr_b, cross_w, cross_b, out):
     nc = tc.nc
+    POOL_M = [m for m in range(M_OUT) if ROUTE[m] == "G"]
     with ExitStack() as ctx:
         const = ctx.enter_context(tc.tile_pool(name="const", bufs=1))
         g_pool = ctx.enter_context(tc.tile_pool(name="g", bufs=6))
@@ -156,6 +157,20 @@ def tile_simplemodel_pb_t_kernel(tc, tok, corr_w, corr_b, cross_w, cross_b, out)
         cross_bias = const.tile([P, E], F32)
         nc.scalar.copy(out=cross_bias[:], in_=xb_ps[:])
 
+        b_sb = const.tile([P, len(POOL_M), P, 2, 2], F32)
+        for gi, m in enumerate(POOL_M):
+            bg_ps = psum_h.tile([P, 2, 2, P], F32, tag="h", name="bg_ps")
+            for eh in range(2):
+                for par in range(2):
+                    codes, scales = w1(1, par, eh)
+                    nc.tensor.matmul_mx(
+                        out=bg_ps[:, eh, par, :], lhsT=codes, lhsT_scale=scales,
+                        rhs=j_codes[:, m * WINDOW : m * WINDOW + P].bitcast(FP8X4),
+                        rhs_scale=j_scales[:, m * WINDOW : m * WINDOW + P],
+                        start=True, stop=True,
+                    )
+            nc.scalar.copy(out=b_sb[:, gi, :, :, :], in_=bg_ps[:].rearrange("p h g c -> p c h g"))
+
         out_rows = out.rearrange("b (x n a) m e -> (b x) n a (m e)", x=2, n=N_BLOCKS, a=2)
 
         units = [(a, n0, m) for a in range(2) for n0 in range(0, N_BLOCKS, 2) for m in range(M_OUT)]
@@ -164,15 +179,26 @@ def tile_simplemodel_pb_t_kernel(tc, tok, corr_w, corr_b, cross_w, cross_b, out)
         banks_of = {}
         rows_of = {}
 
-        def by_vector(k):
-            return k % TURNS in VECTOR_TURNS
-
         def make_h(k):
             a, n0, m = units[k]
-            g_grouped = g_pool.tile([P, WINDOW, 2, 2], BF16, align_bytes=64, tag="g_grouped", name="g_grouped")
-            grouped_of[k] = g_grouped
+            if k % PAIR == 0:
+                grouped_of[k // PAIR] = g_pool.tile(
+                    [P, PAIR * WINDOW, 2, 2], BF16, align_bytes=64, tag="g_grouped", name="g_grouped"
+                )
+            first = (k % PAIR) * WINDOW
+            g_grouped = grouped_of[k // PAIR][:, first : first + WINDOW, :, :]
             j_cols = slice(m * WINDOW, (m + 1) * WINDOW)
-            if by_vector(k):
+            if ROUTE[m] == "G":
+                for l in range(2):
+                    n = n0 + l
+                    stored = a_term[:, a, :, n * P : (n + 1) * P].rearrange("p h c -> p c h")
+                    nc.gpsimd.tensor_tensor(
+                        out=g_grouped[:, l * P : (l + 1) * P, :, :],
+                        in0=b_sb[:, POOL_M.index(m), :, :, :],
+                        in1=stored.unsqueeze(3).to_broadcast([P, P, 2, 2]),
+                        op=ADD,
+                    )
+            elif ROUTE[m] == "V":
                 b_ps = psum_h.tile([P, 2, 2, P], F32, tag="h", name="b_ps")
                 for eh in range(2):
                     for par in range(2):
@@ -215,20 +241,21 @@ def tile_simplemodel_pb_t_kernel(tc, tok, corr_w, corr_b, cross_w, cross_b, out)
                     )
 
         def quantise_g(k):
-            codes = g_pool.tile([P, WINDOW], U32, align_bytes=64, tag="g_codes", name="codes")
-            scales = g_pool.tile([P, WINDOW], U8, align_bytes=64, tag="g_scales", name="scales")
+            codes = g_pool.tile([P, PAIR * WINDOW], U32, align_bytes=64, tag="g_codes", name="codes")
+            scales = g_pool.tile([P, PAIR * WINDOW], U8, align_bytes=64, tag="g_scales", name="scales")
             nc.vector.quantize_mx(
                 out=codes[:].bitcast(FP8X4), scales=scales[:], in_=grouped_of[k][:].rearrange("p c h g -> p (c h g)")
             )
             codes_of[k] = (codes, scales)
 
         def second_matmul(k):
-            codes, scales = codes_of[k]
+            codes, scales = codes_of[k // PAIR]
             o_ps = psum_o.tile([P, 2, E], F32, tag="o", name="o_ps")
             for l in range(2):
+                cols = slice((k % PAIR) * WINDOW + l * P, (k % PAIR) * WINDOW + (l + 1) * P)
                 nc.tensor.matmul_mx(
                     out=o_ps[:, l, :],
-                    lhsT=codes[:, l * P : (l + 1) * P].bitcast(FP8X4), lhsT_scale=scales[:, l * P : (l + 1) * P],
+                    lhsT=codes[:, cols].bitcast(FP8X4), lhsT_scale=scales[:, cols],
                     rhs=w2_codes[:].bitcast(FP8X4), rhs_scale=w2_scales[:],
                     start=True, stop=True,
                 )
@@ -252,12 +279,12 @@ def tile_simplemodel_pb_t_kernel(tc, tok, corr_w, corr_b, cross_w, cross_b, out)
 
         n_units = len(units)
         with tc.manual_schedule():
-            for step in range(n_units + 5):
-                if 0 <= step - 5:
-                    bias_and_store(step - 5)
+            for step in range(n_units + 6):
+                if 0 <= step - 6:
+                    bias_and_store(step - 6)
                 if step < n_units:
                     make_h(step)
-                if 0 <= step - 3 < n_units:
-                    quantise_g(step - 3)
-                if 0 <= step - 4 < n_units:
-                    second_matmul(step - 4)
+                if 0 <= step - 3 < n_units and (step - 3) % PAIR == PAIR - 1:
+                    quantise_g((step - 3) // PAIR)
+                if 0 <= step - 5 < n_units:
+                    second_matmul(step - 5)

@@ -20,8 +20,8 @@ M_OUT = NTOK // 2
 N_BLOCKS = 4
 WINDOW = 2 * P
 M_PER_STORE = 2
-ROUTE = "SSGSSGSG"
-PAIR = 2
+ROUTE = "SSVGSSSG"
+PAIR = 4
 
 FLOPS = 2 * B * NTOK * NTOK * 2 * E * E + 2 * B * NTOK * M_OUT * 2 * E * E
 
@@ -31,7 +31,7 @@ def tile_simplemodel_pb_t_kernel(tc, tok, corr_w, corr_b, cross_w, cross_b, out)
     POOL_M = [m for m in range(M_OUT) if ROUTE[m] == "G"]
     with ExitStack() as ctx:
         const = ctx.enter_context(tc.tile_pool(name="const", bufs=1))
-        g_pool = ctx.enter_context(tc.tile_pool(name="g", bufs=6))
+        g_pool = ctx.enter_context(tc.tile_pool(name="g", bufs=3))
         out_pool = ctx.enter_context(tc.tile_pool(name="rows", bufs=4))
         psum_h = ctx.enter_context(tc.psum_pool(name="psum_h", bufs=6))
         psum_o = ctx.enter_context(tc.psum_pool(name="psum_o", bufs=2))
@@ -279,12 +279,12 @@ def tile_simplemodel_pb_t_kernel(tc, tok, corr_w, corr_b, cross_w, cross_b, out)
 
         n_units = len(units)
         with tc.manual_schedule():
-            for step in range(n_units + 6):
-                if 0 <= step - 6:
-                    bias_and_store(step - 6)
+            for step in range(n_units + 7):
+                if 0 <= step - 7:
+                    bias_and_store(step - 7)
                 if step < n_units:
                     make_h(step)
                 if 0 <= step - 3 < n_units and (step - 3) % PAIR == PAIR - 1:
                     quantise_g((step - 3) // PAIR)
-                if 0 <= step - 5 < n_units:
-                    second_matmul(step - 5)
+                if 0 <= step - 6 < n_units:
+                    second_matmul(step - 6)

@@ -20,8 +20,12 @@ M_OUT = NTOK // 2
 N_BLOCKS = 4
 WINDOW = 2 * P
 M_PER_STORE = 2
-ROUTE = "SSVGSSSG"
+ROUTE = "VGSSSGSS"
 PAIR = 4
+LAG_V = 1
+LAG_Q = 4
+LAG_M = PAIR - 1 + LAG_Q + 1
+LAG_O = LAG_M + 2
 
 FLOPS = 2 * B * NTOK * NTOK * 2 * E * E + 2 * B * NTOK * M_OUT * 2 * E * E
 
@@ -31,11 +35,14 @@ def tile_simplemodel_pb_t_kernel(tc, tok, corr_w, corr_b, cross_w, cross_b, out)
     POOL_M = [m for m in range(M_OUT) if ROUTE[m] == "G"]
     with ExitStack() as ctx:
         const = ctx.enter_context(tc.tile_pool(name="const", bufs=1))
-        g_pool = ctx.enter_context(tc.tile_pool(name="g", bufs=3))
+        g_pool = ctx.enter_context(tc.tile_pool(name="g", bufs=4))
         out_pool = ctx.enter_context(tc.tile_pool(name="rows", bufs=4))
-        psum_h = ctx.enter_context(tc.psum_pool(name="psum_h", bufs=6))
-        psum_o = ctx.enter_context(tc.psum_pool(name="psum_o", bufs=2))
+        psum_h = ctx.enter_context(tc.psum_pool(name="psum_h", bufs=5))
+        psum_o = ctx.enter_context(tc.psum_pool(name="psum_o", bufs=3))
 
+        warm = const.tile([P, 2], F32)
+        nc.gpsimd.memset(warm[:], 0.0)
+        nc.scalar.activation(out=warm[:, 1:2], in_=warm[:, 0:1], func=IDENTITY, scale=1.0)
         ident_f32 = const.tile([P, P], F32)
         make_identity(nc, ident_f32[:])
         ident_bf = const.tile([P, P], BF16)
@@ -92,7 +99,7 @@ def tile_simplemodel_pb_t_kernel(tc, tok, corr_w, corr_b, cross_w, cross_b, out)
                 for u in range(2):
                     nc.tensor.transpose(xt[:, nb, u, :], tok_words[:, 2 * pair + nb, u, :], ident_f32[:])
             xts.append(xt)
-        wct = psum_h.tile([P, PACK, E], BF16, tag="h")
+        wct = psum_o.tile([P, PACK, E], BF16, tag="o")
         for eh in range(2):
             for par in range(2):
                 for hh in range(2):
@@ -100,9 +107,9 @@ def tile_simplemodel_pb_t_kernel(tc, tok, corr_w, corr_b, cross_w, cross_b, out)
                     nc.tensor.transpose(
                         wct[:, 2 * eh + par, hh * P : (hh + 1) * P], xw_sb[:, hh, first : first + P], ident_bf[:]
                     )
-        cbt = psum_h.tile([P, P], BF16, tag="h")
+        cbt = psum_o.tile([P, P], BF16, tag="o")
         nc.tensor.transpose(cbt[:], bias_rows[:, 0:P], ident_bf[:])
-        xb_ps = psum_h.tile([P, E], F32, tag="h")
+        xb_ps = psum_o.tile([P, E], F32, tag="o")
         nc.tensor.matmul(out=xb_ps[:], lhsT=ones[:], rhs=bias_rows[:, P : P + E], start=True, stop=True)
         corr_bias = const.tile([P, 2], F32)
         nc.vector.tensor_copy(out=corr_bias[:], in_=cbt[:, 0:2])
@@ -115,23 +122,21 @@ def tile_simplemodel_pb_t_kernel(tc, tok, corr_w, corr_b, cross_w, cross_b, out)
             )
         i_codes = const.tile([P, N_BLOCKS * P], U32, align_bytes=64)
         i_scales = const.tile([P, N_BLOCKS * P], U8, align_bytes=64)
+        nc.vector.memset(i_scales[:].bitcast(I32), 0)
         nc.vector.quantize_mx(out=i_codes[:].bitcast(FP8X4), scales=i_scales[:], in_=i_grouped[:])
 
-        j_grouped = const.tile([P, M_OUT * WINDOW * PACK], BF16, align_bytes=64)
-        j_words = j_grouped[:].bitcast(F32).rearrange("p (m l b d u) -> p m l b d u", m=M_OUT, l=2, d=2, u=2)
-        j_codes = const.tile([P, M_OUT * WINDOW], U32, align_bytes=64)
-        j_scales = const.tile([P, M_OUT * WINDOW], U8, align_bytes=64)
-        for m in range(M_OUT):
-            n, x = m % N_BLOCKS, m // N_BLOCKS
-            src = xts[n // 2][:, n % 2, :, :].rearrange("p u (b x) -> p x b u", x=2)[:, x, :, :]
-            src = src.unsqueeze(2).to_broadcast([P, B, 2, 2])
-            nc.scalar.copy(out=j_words[:, m, 0, :, :, :], in_=src)
-            nc.vector.tensor_copy(out=j_words[:, m, 1, :, :, :], in_=src)
-            cols = slice(m * WINDOW, (m + 1) * WINDOW)
-            nc.vector.quantize_mx(
-                out=j_codes[:, cols].bitcast(FP8X4),
-                scales=j_scales[:, cols],
-                in_=j_grouped[:, m * WINDOW * PACK : (m + 1) * WINDOW * PACK],
+        j_codes = const.tile([P, M_OUT * P], U32, align_bytes=64)
+        j_scales = const.tile([P, M_OUT * P], U8, align_bytes=64)
+        i_code_cols = i_codes[:].bitcast(I32).rearrange("p (n b x) -> p x n b", n=N_BLOCKS, x=2)
+        j_code_cols = j_codes[:].bitcast(I32).rearrange("p (x n b d) -> p x n b d", x=2, n=N_BLOCKS, d=2)
+        for x in range(2):
+            nc.vector.tensor_copy(
+                out=j_code_cols[:, x, :, :, :], in_=i_code_cols[:, x, :, :].unsqueeze(3).to_broadcast([P, N_BLOCKS, B, 2])
+            )
+        j_scale_cols = j_scales[:].rearrange("p (x n b d) -> p n b x d", x=2, n=N_BLOCKS, d=2)
+        for d in range(2):
+            nc.vector.tensor_copy(
+                out=j_scale_cols[:, :, :, :, d], in_=i_scales[:].rearrange("p (n b x) -> p n b x", n=N_BLOCKS, x=2)
             )
 
         a_term = const.tile([P, 2, 2, N_BLOCKS * P], F32)
@@ -165,8 +170,8 @@ def tile_simplemodel_pb_t_kernel(tc, tok, corr_w, corr_b, cross_w, cross_b, out)
                     codes, scales = w1(1, par, eh)
                     nc.tensor.matmul_mx(
                         out=bg_ps[:, eh, par, :], lhsT=codes, lhsT_scale=scales,
-                        rhs=j_codes[:, m * WINDOW : m * WINDOW + P].bitcast(FP8X4),
-                        rhs_scale=j_scales[:, m * WINDOW : m * WINDOW + P],
+                        rhs=j_codes[:, m * P : (m + 1) * P].bitcast(FP8X4),
+                        rhs_scale=j_scales[:, m * P : (m + 1) * P],
                         start=True, stop=True,
                     )
             nc.scalar.copy(out=b_sb[:, gi, :, :, :], in_=bg_ps[:].rearrange("p h g c -> p c h g"))
@@ -175,6 +180,7 @@ def tile_simplemodel_pb_t_kernel(tc, tok, corr_w, corr_b, cross_w, cross_b, out)
 
         units = [(a, n0, m) for a in range(2) for n0 in range(0, N_BLOCKS, 2) for m in range(M_OUT)]
         grouped_of = {}
+        b_of = {}
         codes_of = {}
         banks_of = {}
         rows_of = {}
@@ -187,7 +193,7 @@ def tile_simplemodel_pb_t_kernel(tc, tok, corr_w, corr_b, cross_w, cross_b, out)
                 )
             first = (k % PAIR) * WINDOW
             g_grouped = grouped_of[k // PAIR][:, first : first + WINDOW, :, :]
-            j_cols = slice(m * WINDOW, (m + 1) * WINDOW)
+            j_cols = slice(m * P, (m + 1) * P)
             if ROUTE[m] == "G":
                 for l in range(2):
                     n = n0 + l
@@ -205,19 +211,11 @@ def tile_simplemodel_pb_t_kernel(tc, tok, corr_w, corr_b, cross_w, cross_b, out)
                         codes, scales = w1(1, par, eh)
                         nc.tensor.matmul_mx(
                             out=b_ps[:, eh, par, :], lhsT=codes, lhsT_scale=scales,
-                            rhs=j_codes[:, m * WINDOW : m * WINDOW + P].bitcast(FP8X4),
-                            rhs_scale=j_scales[:, m * WINDOW : m * WINDOW + P],
+                            rhs=j_codes[:, m * P : (m + 1) * P].bitcast(FP8X4),
+                            rhs_scale=j_scales[:, m * P : (m + 1) * P],
                             start=True, stop=True,
                         )
-                for l in range(2):
-                    n = n0 + l
-                    stored = a_term[:, a, :, n * P : (n + 1) * P].rearrange("p h c -> p c h")
-                    nc.vector.tensor_tensor(
-                        out=g_grouped[:, l * P : (l + 1) * P, :, :],
-                        in0=b_ps[:].rearrange("p h g c -> p c h g"),
-                        in1=stored.unsqueeze(3).to_broadcast([P, P, 2, 2]),
-                        op=ADD,
-                    )
+                b_of[k] = b_ps
             else:
                 for eh in range(2):
                     h_ps = psum_h.tile([P, 2, WINDOW], F32, tag="h", name="h_ps")
@@ -230,15 +228,30 @@ def tile_simplemodel_pb_t_kernel(tc, tok, corr_w, corr_b, cross_w, cross_b, out)
                             start=True, stop=False,
                         )
                         codes, scales = w1(1, par, eh)
-                        nc.tensor.matmul_mx(
-                            out=h_ps[:, par, :], lhsT=codes, lhsT_scale=scales,
-                            rhs=j_codes[:, j_cols].bitcast(FP8X4), rhs_scale=j_scales[:, j_cols],
-                            start=False, stop=True,
-                        )
+                        for l in range(2):
+                            nc.tensor.matmul_mx(
+                                out=h_ps[:, par, l * P : (l + 1) * P], lhsT=codes, lhsT_scale=scales,
+                                rhs=j_codes[:, j_cols].bitcast(FP8X4), rhs_scale=j_scales[:, j_cols],
+                                start=False, stop=(l == 1),
+                            )
                     nc.scalar.activation(
                         out=g_grouped[:, :, eh, :], in_=h_ps[:].rearrange("p g c -> p c g"),
                         func=IDENTITY, bias=corr_bias[:, eh : eh + 1], scale=1.0,
                     )
+
+        def vector_h(k):
+            a, n0, m = units[k]
+            first = (k % PAIR) * WINDOW
+            g_grouped = grouped_of[k // PAIR][:, first : first + WINDOW, :, :]
+            for l in range(2):
+                n = n0 + l
+                stored = a_term[:, a, :, n * P : (n + 1) * P].rearrange("p h c -> p c h")
+                nc.vector.tensor_tensor(
+                    out=g_grouped[:, l * P : (l + 1) * P, :, :],
+                    in0=b_of[k][:].rearrange("p h g c -> p c h g"),
+                    in1=stored.unsqueeze(3).to_broadcast([P, P, 2, 2]),
+                    op=ADD,
+                )
 
         def quantise_g(k):
             codes = g_pool.tile([P, PAIR * WINDOW], U32, align_bytes=64, tag="g_codes", name="codes")
@@ -279,12 +292,14 @@ def tile_simplemodel_pb_t_kernel(tc, tok, corr_w, corr_b, cross_w, cross_b, out)
 
         n_units = len(units)
         with tc.manual_schedule():
-            for step in range(n_units + 7):
-                if 0 <= step - 7:
-                    bias_and_store(step - 7)
+            for step in range(n_units + LAG_O):
+                if 0 <= step - LAG_O:
+                    bias_and_store(step - LAG_O)
                 if step < n_units:
                     make_h(step)
-                if 0 <= step - 3 < n_units and (step - 3) % PAIR == PAIR - 1:
-                    quantise_g((step - 3) // PAIR)
-                if 0 <= step - 6 < n_units:
-                    second_matmul(step - 6)
+                if 0 <= step - LAG_V < n_units and ROUTE[units[step - LAG_V][2]] == "V":
+                    vector_h(step - LAG_V)
+                if 0 <= step - LAG_Q < n_units and (step - LAG_Q) % PAIR == PAIR - 1:
+                    quantise_g((step - LAG_Q) // PAIR)
+                if 0 <= step - LAG_M < n_units:
+                    second_matmul(step - LAG_M)

@@ -21,10 +21,9 @@ N_BLOCKS = 4
 WINDOW = 2 * P
 M_PER_STORE = 2
 ROUTE = "VGSSSGSS"
-PAIR = 4
+GROUPS = [4, 4, 4, 4, 4, 4, 4, 2, 1, 1]
 LAG_V = 1
-LAG_Q = 4
-LAG_M = PAIR - 1 + LAG_Q + 1
+LAG_M = 8
 LAG_O = LAG_M + 2
 
 FLOPS = 2 * B * NTOK * NTOK * 2 * E * E + 2 * B * NTOK * M_OUT * 2 * E * E
@@ -148,9 +147,14 @@ def tile_simplemodel_pb_t_kernel(tc, tok, corr_w, corr_b, cross_w, cross_b, out)
                     out=a_ps[:], lhsT=codes, lhsT_scale=scales, rhs=i_codes[:].bitcast(FP8X4), rhs_scale=i_scales[:],
                     start=True, stop=True,
                 )
-                nc.scalar.activation(
-                    out=a_term[:, a, eh, :], in_=a_ps[:], func=IDENTITY, bias=corr_bias[:, eh : eh + 1], scale=1.0
-                )
+                if a == 0:
+                    nc.scalar.activation(
+                        out=a_term[:, a, eh, :], in_=a_ps[:], func=IDENTITY, bias=corr_bias[:, eh : eh + 1], scale=1.0
+                    )
+                else:
+                    nc.vector.tensor_scalar(
+                        out=a_term[:, a, eh, :], in0=a_ps[:], scalar1=corr_bias[:, eh : eh + 1], scalar2=None, op0=ADD
+                    )
 
         w2_grouped = const.tile([P, E, PACK], BF16, align_bytes=64)
         nc.scalar.copy(out=w2_grouped[:], in_=wct[:].rearrange("p t e -> p e t"))
@@ -160,7 +164,7 @@ def tile_simplemodel_pb_t_kernel(tc, tok, corr_w, corr_b, cross_w, cross_b, out)
             out=w2_codes[:].bitcast(FP8X4), scales=w2_scales[:], in_=w2_grouped[:].rearrange("p e t -> p (e t)")
         )
         cross_bias = const.tile([P, E], F32)
-        nc.scalar.copy(out=cross_bias[:], in_=xb_ps[:])
+        nc.vector.tensor_copy(out=cross_bias[:], in_=xb_ps[:])
 
         b_sb = const.tile([P, len(POOL_M), P, 2, 2], F32)
         for gi, m in enumerate(POOL_M):
@@ -174,11 +178,16 @@ def tile_simplemodel_pb_t_kernel(tc, tok, corr_w, corr_b, cross_w, cross_b, out)
                         rhs_scale=j_scales[:, m * P : (m + 1) * P],
                         start=True, stop=True,
                     )
-            nc.scalar.copy(out=b_sb[:, gi, :, :, :], in_=bg_ps[:].rearrange("p h g c -> p c h g"))
+            nc.vector.tensor_copy(out=b_sb[:, gi, :, :, :], in_=bg_ps[:].rearrange("p h g c -> p c h g"))
 
         out_rows = out.rearrange("b (x n a) m e -> (b x) n a (m e)", x=2, n=N_BLOCKS, a=2)
 
         units = [(a, n0, m) for a in range(2) for n0 in range(0, N_BLOCKS, 2) for m in range(M_OUT)]
+        group_of = []
+        first_of = []
+        for p, size in enumerate(GROUPS):
+            first_of.append(len(group_of))
+            group_of.extend([p] * size)
         grouped_of = {}
         b_of = {}
         codes_of = {}
@@ -187,12 +196,13 @@ def tile_simplemodel_pb_t_kernel(tc, tok, corr_w, corr_b, cross_w, cross_b, out)
 
         def make_h(k):
             a, n0, m = units[k]
-            if k % PAIR == 0:
-                grouped_of[k // PAIR] = g_pool.tile(
-                    [P, PAIR * WINDOW, 2, 2], BF16, align_bytes=64, tag="g_grouped", name="g_grouped"
+            p = group_of[k]
+            if k == first_of[p]:
+                grouped_of[p] = g_pool.tile(
+                    [P, GROUPS[p] * WINDOW, 2, 2], BF16, align_bytes=64, tag="g_grouped", name="g_grouped"
                 )
-            first = (k % PAIR) * WINDOW
-            g_grouped = grouped_of[k // PAIR][:, first : first + WINDOW, :, :]
+            first = (k - first_of[p]) * WINDOW
+            g_grouped = grouped_of[p][:, first : first + WINDOW, :, :]
             j_cols = slice(m * P, (m + 1) * P)
             if ROUTE[m] == "G":
                 for l in range(2):
@@ -241,8 +251,8 @@ def tile_simplemodel_pb_t_kernel(tc, tok, corr_w, corr_b, cross_w, cross_b, out)
 
         def vector_h(k):
             a, n0, m = units[k]
-            first = (k % PAIR) * WINDOW
-            g_grouped = grouped_of[k // PAIR][:, first : first + WINDOW, :, :]
+            first = (k - first_of[group_of[k]]) * WINDOW
+            g_grouped = grouped_of[group_of[k]][:, first : first + WINDOW, :, :]
             for l in range(2):
                 n = n0 + l
                 stored = a_term[:, a, :, n * P : (n + 1) * P].rearrange("p h c -> p c h")
@@ -254,18 +264,19 @@ def tile_simplemodel_pb_t_kernel(tc, tok, corr_w, corr_b, cross_w, cross_b, out)
                 )
 
         def quantise_g(k):
-            codes = g_pool.tile([P, PAIR * WINDOW], U32, align_bytes=64, tag="g_codes", name="codes")
-            scales = g_pool.tile([P, PAIR * WINDOW], U8, align_bytes=64, tag="g_scales", name="scales")
+            codes = g_pool.tile([P, GROUPS[k] * WINDOW], U32, align_bytes=64, tag="g_codes", name="codes")
+            scales = g_pool.tile([P, GROUPS[k] * WINDOW], U8, align_bytes=64, tag="g_scales", name="scales")
             nc.vector.quantize_mx(
                 out=codes[:].bitcast(FP8X4), scales=scales[:], in_=grouped_of[k][:].rearrange("p c h g -> p (c h g)")
             )
             codes_of[k] = (codes, scales)
 
         def second_matmul(k):
-            codes, scales = codes_of[k // PAIR]
+            codes, scales = codes_of[group_of[k]]
+            first = (k - first_of[group_of[k]]) * WINDOW
             o_ps = psum_o.tile([P, 2, E], F32, tag="o", name="o_ps")
             for l in range(2):
-                cols = slice((k % PAIR) * WINDOW + l * P, (k % PAIR) * WINDOW + (l + 1) * P)
+                cols = slice(first + l * P, first + (l + 1) * P)
                 nc.tensor.matmul_mx(
                     out=o_ps[:, l, :],
                     lhsT=codes[:, cols].bitcast(FP8X4), lhsT_scale=scales[:, cols],
@@ -293,13 +304,13 @@ def tile_simplemodel_pb_t_kernel(tc, tok, corr_w, corr_b, cross_w, cross_b, out)
         n_units = len(units)
         with tc.manual_schedule():
             for step in range(n_units + LAG_O):
+                if step - LAG_M in first_of:
+                    quantise_g(first_of.index(step - LAG_M))
                 if 0 <= step - LAG_O:
                     bias_and_store(step - LAG_O)
                 if step < n_units:
                     make_h(step)
                 if 0 <= step - LAG_V < n_units and ROUTE[units[step - LAG_V][2]] == "V":
                     vector_h(step - LAG_V)
-                if 0 <= step - LAG_Q < n_units and (step - LAG_Q) % PAIR == PAIR - 1:
-                    quantise_g((step - LAG_Q) // PAIR)
                 if 0 <= step - LAG_M < n_units:
                     second_matmul(step - LAG_M)

@@ -128,15 +128,14 @@ def tile_simplemodel_pb_t_kernel(tc, tok, corr_w, corr_b, cross_w, cross_b, out)
         j_scales = const.tile([P, M_OUT * P], U8, align_bytes=64)
         i_code_cols = i_codes[:].bitcast(I32).rearrange("p (n b x) -> p x n b", n=N_BLOCKS, x=2)
         j_code_cols = j_codes[:].bitcast(I32).rearrange("p (x n b d) -> p x n b d", x=2, n=N_BLOCKS, d=2)
-        for x in range(2):
-            nc.vector.tensor_copy(
+        i_scale_cols = i_scales[:].rearrange("p (n b x) -> p x n b", n=N_BLOCKS, x=2)
+        j_scale_cols = j_scales[:].rearrange("p (x n b d) -> p x d n b", x=2, n=N_BLOCKS, d=2)
+        for x, engine in ((0, nc.vector), (1, nc.gpsimd)):
+            engine.tensor_copy(
                 out=j_code_cols[:, x, :, :, :], in_=i_code_cols[:, x, :, :].unsqueeze(3).to_broadcast([P, N_BLOCKS, B, 2])
             )
-        j_scale_cols = j_scales[:].rearrange("p (x n b d) -> p n b x d", x=2, n=N_BLOCKS, d=2)
-        for d in range(2):
-            nc.vector.tensor_copy(
-                out=j_scale_cols[:, :, :, :, d], in_=i_scales[:].rearrange("p (n b x) -> p n b x", n=N_BLOCKS, x=2)
-            )
+            for d in range(2):
+                engine.tensor_copy(out=j_scale_cols[:, x, d, :, :], in_=i_scale_cols[:, x, :, :])
 
         a_term = const.tile([P, 2, 2, N_BLOCKS * P], F32)
         for a in range(2):

@@ -204,15 +204,13 @@ def tile_simplemodel_pb_t_kernel(tc, tok, corr_w, corr_b, cross_w, cross_b, out)
             g_grouped = grouped_of[p][:, first : first + WINDOW, :, :]
             j_cols = slice(m * P, (m + 1) * P)
             if ROUTE[m] == "G":
-                for l in range(2):
-                    n = n0 + l
-                    stored = a_term[:, a, :, n * P : (n + 1) * P].rearrange("p h c -> p c h")
-                    nc.gpsimd.tensor_tensor(
-                        out=g_grouped[:, l * P : (l + 1) * P, :, :],
-                        in0=b_sb[:, POOL_M.index(m), :, :, :],
-                        in1=stored.unsqueeze(3).to_broadcast([P, P, 2, 2]),
-                        op=ADD,
-                    )
+                stored = a_term[:, a, :, n0 * P : (n0 + 2) * P].rearrange("p h (l c) -> p l c h", l=2)
+                nc.gpsimd.tensor_tensor(
+                    out=g_grouped.rearrange("p (l c) h g -> p l c h g", l=2),
+                    in0=b_sb[:, POOL_M.index(m), :, :, :].unsqueeze(1).to_broadcast([P, 2, P, 2, 2]),
+                    in1=stored.unsqueeze(4).to_broadcast([P, 2, P, 2, 2]),
+                    op=ADD,
+                )
             elif ROUTE[m] == "V":
                 b_ps = psum_h.tile([P, 2, 2, P], F32, tag="h", name="b_ps")
                 for eh in range(2):

@@ -31,66 +31,55 @@ FLOPS = 2 * B * NTOK * NTOK * 2 * E * E + 2 * B * NTOK * M_OUT * 2 * E * E
 
 def tile_simplemodel_pb_t_kernel(tc, tok, corr_w, corr_b, cross_w, cross_b, out):
     nc = tc.nc
-    POOL_M = [m for m in range(M_OUT) if ROUTE[m] == "G"]
     with ExitStack() as ctx:
         const = ctx.enter_context(tc.tile_pool(name="const", bufs=1))
-        g_pool = ctx.enter_context(tc.tile_pool(name="g", bufs=4))
+        g_pool = ctx.enter_context(tc.tile_pool(name="g", bufs=6))
         out_pool = ctx.enter_context(tc.tile_pool(name="rows", bufs=4))
         psum_h = ctx.enter_context(tc.psum_pool(name="psum_h", bufs=5))
         psum_o = ctx.enter_context(tc.psum_pool(name="psum_o", bufs=3))
+        ctx.enter_context(tc.manual_schedule())
 
-        warm = const.tile([P, 2], F32)
-        nc.gpsimd.memset(warm[:], 0.0)
-        nc.scalar.activation(out=warm[:, 1:2], in_=warm[:, 0:1], func=IDENTITY, scale=1.0)
-        ident_f32 = const.tile([P, P], F32)
-        make_identity(nc, ident_f32[:])
-        ident_bf = const.tile([P, P], BF16)
-        nc.vector.tensor_copy(out=ident_bf[:], in_=ident_f32[:])
+        cw_sb = const.tile([P, 2, 2 * E], BF16)
+        nc.sync.dma_start(out=cw_sb[:], in_=corr_w.rearrange("(h p) k -> p h k", p=P))
         tok_sb = const.tile([P, 8 * E], BF16)
         tok_rows = tok.rearrange("b (x r) k -> (b x) (r k)", x=2)
         nc.sync.dma_start(out=tok_sb[:, 0 : 4 * E], in_=tok_rows[:, 0 : 4 * E])
         nc.sync.dma_start(out=tok_sb[:, 4 * E : 8 * E], in_=tok_rows[:, 4 * E : 8 * E])
-        cw_sb = const.tile([P, 2, 2, 2 * E], BF16)
-        cw_rows = corr_w.rearrange("(h p) k -> p h k", p=P)
-        nc.scalar.dma_start(out=cw_sb[:, 0, :, :], in_=cw_rows)
-        nc.scalar.dma_start(out=cw_sb[:, 1, :, 0:E], in_=cw_rows[:, :, E : 2 * E])
-        nc.scalar.dma_start(out=cw_sb[:, 1, :, E : 2 * E], in_=cw_rows[:, :, 0:E])
+        warm = const.tile([P, 2], F32)
+        nc.vector.memset(warm[:], 0.0)
+        nc.scalar.activation(out=warm[:, 1:2], in_=warm[:, 0:1], func=IDENTITY, scale=1.0)
+        ident_f32 = const.tile([P, P], F32)
+        make_identity(nc, ident_f32[:])
         bias_rows = const.tile([P, P + E], BF16)
         nc.vector.memset(bias_rows[:], 0.0)
         nc.sync.dma_start(out=bias_rows[0:2, 0:P], in_=corr_b.rearrange("(h e) -> h e", h=2))
         nc.sync.dma_start(out=bias_rows[0:1, P : P + E], in_=cross_b.rearrange("(o e) -> o e", o=1))
+        xw_sb = const.tile([P, 2, 2 * E], BF16)
+        nc.sync.dma_start(out=xw_sb[:], in_=cross_w.rearrange("(h p) k -> p h k", p=P))
         ones = const.tile([P, P], BF16)
         nc.vector.memset(ones[:], 1.0)
-        xw_sb = const.tile([P, 2, 2 * E], BF16)
-        nc.scalar.dma_start(out=xw_sb[:], in_=cross_w.rearrange("(h p) k -> p h k", p=P))
+        w1_codes = const.tile([P, 4, 2 * P], U32, align_bytes=64)
+        w1_scales = const.tile([P, 4, 2 * P], U8, align_bytes=64)
+        nc.vector.memset(w1_codes[:].bitcast(I32), 0)
+        nc.vector.memset(w1_scales[:].bitcast(I32), 0)
+        i_scales = const.tile([P, N_BLOCKS * P], U8, align_bytes=64)
+        nc.vector.memset(i_scales[:].bitcast(I32), 0)
+        w_scales = const.tile([P, 2 * P], U8, align_bytes=64)
+        nc.vector.memset(w_scales[:].bitcast(I32), 0)
+        ident_bf = const.tile([P, P], BF16)
+        nc.vector.tensor_copy(out=ident_bf[:], in_=ident_f32[:])
 
-        w1_grouped = const.tile([P, 8 * P * PACK], BF16, align_bytes=64)
-        nc.vector.memset(w1_grouped[:].bitcast(I32), 0)
-        w1_words = w1_grouped[:].bitcast(F32).rearrange("p (v e u) -> p v e u", v=8, u=2)
-        cw_words = cw_sb[:].rearrange("p s h k -> p (s h k)").bitcast(F32).rearrange("p (v q u) -> p v u q", v=4, u=2)
-        for s in range(2):
-            wt = psum_h.tile([P, 2, 2, P], F32, tag="h")
-            for eh in range(2):
-                for u in range(2):
-                    nc.tensor.transpose(wt[:, eh, u, :], cw_words[:, 2 * s + eh, u, :], ident_f32[:])
-            for half in range(2):
-                kind = half if s == 0 else 1 - half
-                v = 4 * kind + 2 * half
-                rows = slice(HALF * half, HALF * (half + 1))
-                src = wt[rows].rearrange("p h u e -> p h e u")
-                if s == 0:
-                    nc.scalar.copy(out=w1_words[rows, v : v + 2, :, :], in_=src)
-                else:
-                    nc.vector.tensor_copy(out=w1_words[rows, v : v + 2, :, :], in_=src)
-        w1_codes = const.tile([P, 8 * P], U32, align_bytes=64)
-        w1_scales = const.tile([P, 8 * P], U8, align_bytes=64)
-        nc.vector.quantize_mx(out=w1_codes[:].bitcast(FP8X4), scales=w1_scales[:], in_=w1_grouped[:])
-
-        def w1(kind, half, eh):
-            v = 4 * kind + 2 * half + eh
-            return w1_codes[:, v * P : (v + 1) * P].bitcast(FP8X4), w1_scales[:, v * P : (v + 1) * P]
-
+        cw_words = cw_sb[:].rearrange("p h k -> p (h k)").bitcast(F32).rearrange("p (h q u) -> p h u q", h=2, u=2)
+        wt = psum_h.tile([P, 2, 2, P], F32, tag="h", name="wt")
+        for eh in range(2):
+            for u in range(2):
+                nc.tensor.transpose(wt[:, eh, u, :], cw_words[:, eh, u, :], ident_f32[:])
+        w_grouped = const.tile([P, 2 * P * PACK], BF16, align_bytes=64)
+        w_words = w_grouped[:].bitcast(F32).rearrange("p (h e u) -> p h e u", h=2, u=2)
+        nc.scalar.copy(out=w_words, in_=wt[:].rearrange("p h u e -> p h e u"))
         tok_words = tok_sb[:].bitcast(F32).rearrange("p (n q u) -> p n u q", n=N_BLOCKS, u=2)
+        i_grouped = const.tile([P, N_BLOCKS * P * PACK], BF16, align_bytes=64)
+        i_words = i_grouped[:].bitcast(F32).rearrange("p (n c u) -> p n c u", n=N_BLOCKS, u=2)
         xts = []
         for pair in range(2):
             xt = psum_h.tile([P, 2, 2, P], F32, tag="h", name="xt%d" % pair)
@@ -98,6 +87,23 @@ def tile_simplemodel_pb_t_kernel(tc, tok, corr_w, corr_b, cross_w, cross_b, out)
                 for u in range(2):
                     nc.tensor.transpose(xt[:, nb, u, :], tok_words[:, 2 * pair + nb, u, :], ident_f32[:])
             xts.append(xt)
+        w_codes = const.tile([P, 2 * P], U32, align_bytes=64)
+        nc.vector.quantize_mx(out=w_codes[:].bitcast(FP8X4), scales=w_scales[:], in_=w_grouped[:])
+        for kind, half in ((0, 0), (1, 0), (1, 1), (0, 1)):
+            rows = slice(HALF * half, HALF * (half + 1))
+            source = slice(HALF * kind, HALF * (kind + 1))
+            v = 2 * kind + half
+            nc.sync.dma_start(out=w1_codes[rows, v, :].bitcast(I32), in_=w_codes[source, :].bitcast(I32))
+            nc.sync.dma_start(out=w1_scales[rows, v, :].bitcast(I32), in_=w_scales[source, :].bitcast(I32))
+
+        def w1(kind, half, eh):
+            v = 2 * kind + half
+            cols = slice(eh * P, (eh + 1) * P)
+            return w1_codes[:, v, cols].bitcast(FP8X4), w1_scales[:, v, cols]
+
+        i_codes = const.tile([P, N_BLOCKS * P], U32, align_bytes=64)
+        for pair, copy in ((0, nc.scalar.copy), (1, nc.vector.tensor_copy)):
+            copy(out=i_words[:, 2 * pair : 2 * pair + 2, :, :], in_=xts[pair][:].rearrange("p n u c -> p n c u"))
         wct = psum_o.tile([P, PACK, E], BF16, tag="o")
         for eh in range(2):
             for par in range(2):
@@ -110,19 +116,12 @@ def tile_simplemodel_pb_t_kernel(tc, tok, corr_w, corr_b, cross_w, cross_b, out)
         nc.tensor.transpose(cbt[:], bias_rows[:, 0:P], ident_bf[:])
         xb_ps = psum_o.tile([P, E], F32, tag="o")
         nc.tensor.matmul(out=xb_ps[:], lhsT=ones[:], rhs=bias_rows[:, P : P + E], start=True, stop=True)
+        w2_grouped = const.tile([P, E, PACK], BF16, align_bytes=64)
+        nc.scalar.copy(out=w2_grouped[:], in_=wct[:].rearrange("p t e -> p e t"))
+
+        nc.vector.quantize_mx(out=i_codes[:].bitcast(FP8X4), scales=i_scales[:], in_=i_grouped[:])
         corr_bias = const.tile([P, 2], F32)
         nc.vector.tensor_copy(out=corr_bias[:], in_=cbt[:, 0:2])
-
-        i_grouped = const.tile([P, N_BLOCKS * P * PACK], BF16, align_bytes=64)
-        i_words = i_grouped[:].bitcast(F32).rearrange("p (n c u) -> p n c u", n=N_BLOCKS, u=2)
-        for pair in range(2):
-            nc.scalar.copy(
-                out=i_words[:, 2 * pair : 2 * pair + 2, :, :], in_=xts[pair][:].rearrange("p n u c -> p n c u")
-            )
-        i_codes = const.tile([P, N_BLOCKS * P], U32, align_bytes=64)
-        i_scales = const.tile([P, N_BLOCKS * P], U8, align_bytes=64)
-        nc.vector.memset(i_scales[:].bitcast(I32), 0)
-        nc.vector.quantize_mx(out=i_codes[:].bitcast(FP8X4), scales=i_scales[:], in_=i_grouped[:])
 
         j_codes = const.tile([P, M_OUT * P], U32, align_bytes=64)
         j_scales = const.tile([P, M_OUT * P], U8, align_bytes=64)
@@ -130,54 +129,53 @@ def tile_simplemodel_pb_t_kernel(tc, tok, corr_w, corr_b, cross_w, cross_b, out)
         j_code_cols = j_codes[:].bitcast(I32).rearrange("p (x n b d) -> p x n b d", x=2, n=N_BLOCKS, d=2)
         i_scale_cols = i_scales[:].rearrange("p (n b x) -> p x n b", n=N_BLOCKS, x=2)
         j_scale_cols = j_scales[:].rearrange("p (x n b d) -> p x d n b", x=2, n=N_BLOCKS, d=2)
-        for x, engine in ((0, nc.vector), (1, nc.gpsimd)):
+
+        def move_windows(x, engine):
             engine.tensor_copy(
                 out=j_code_cols[:, x, :, :, :], in_=i_code_cols[:, x, :, :].unsqueeze(3).to_broadcast([P, N_BLOCKS, B, 2])
             )
             for d in range(2):
                 engine.tensor_copy(out=j_scale_cols[:, x, d, :, :], in_=i_scale_cols[:, x, :, :])
 
+        move_windows(0, nc.vector)
+
         a_term = const.tile([P, 2, 2, N_BLOCKS * P], F32)
-        for a in range(2):
-            for eh in range(2):
-                a_ps = psum_h.tile([P, N_BLOCKS * P], F32, tag="h", name="a_ps")
-                codes, scales = w1(0, a, eh)
-                nc.tensor.matmul_mx(
-                    out=a_ps[:], lhsT=codes, lhsT_scale=scales, rhs=i_codes[:].bitcast(FP8X4), rhs_scale=i_scales[:],
-                    start=True, stop=True,
+
+        def make_a_term(a, eh, engine):
+            a_ps = psum_h.tile([P, N_BLOCKS * P], F32, tag="h", name="a_ps")
+            codes, scales = w1(0, a, eh)
+            nc.tensor.matmul_mx(
+                out=a_ps[:], lhsT=codes, lhsT_scale=scales, rhs=i_codes[:].bitcast(FP8X4), rhs_scale=i_scales[:],
+                start=True, stop=True,
+            )
+            if engine == "S":
+                nc.scalar.activation(
+                    out=a_term[:, a, eh, :], in_=a_ps[:], func=IDENTITY, bias=corr_bias[:, eh : eh + 1], scale=1.0
                 )
-                if a == 0:
-                    nc.scalar.activation(
-                        out=a_term[:, a, eh, :], in_=a_ps[:], func=IDENTITY, bias=corr_bias[:, eh : eh + 1], scale=1.0
-                    )
-                else:
-                    nc.vector.tensor_scalar(
-                        out=a_term[:, a, eh, :], in0=a_ps[:], scalar1=corr_bias[:, eh : eh + 1], scalar2=None, op0=ADD
-                    )
+            else:
+                nc.vector.tensor_scalar(
+                    out=a_term[:, a, eh, :], in0=a_ps[:], scalar1=corr_bias[:, eh : eh + 1], scalar2=None, op0=ADD
+                )
 
-        w2_grouped = const.tile([P, E, PACK], BF16, align_bytes=64)
-        nc.scalar.copy(out=w2_grouped[:], in_=wct[:].rearrange("p t e -> p e t"))
-        w2_codes = const.tile([P, E], U32, align_bytes=64)
-        w2_scales = const.tile([P, E], U8, align_bytes=64)
-        nc.vector.quantize_mx(
-            out=w2_codes[:].bitcast(FP8X4), scales=w2_scales[:], in_=w2_grouped[:].rearrange("p e t -> p (e t)")
-        )
-        cross_bias = const.tile([P, E], F32)
-        nc.vector.tensor_copy(out=cross_bias[:], in_=xb_ps[:])
-
+        POOL_M = [1, 5]
         b_sb = const.tile([P, len(POOL_M), P, 2, 2], F32)
-        for gi, m in enumerate(POOL_M):
-            bg_ps = psum_h.tile([P, 2, 2, P], F32, tag="h", name="bg_ps")
+
+        def tok_j_term(m):
+            b_ps = psum_h.tile([P, 2, 2, P], F32, tag="h", name="b_ps")
             for eh in range(2):
                 for par in range(2):
                     codes, scales = w1(1, par, eh)
                     nc.tensor.matmul_mx(
-                        out=bg_ps[:, eh, par, :], lhsT=codes, lhsT_scale=scales,
+                        out=b_ps[:, eh, par, :], lhsT=codes, lhsT_scale=scales,
                         rhs=j_codes[:, m * P : (m + 1) * P].bitcast(FP8X4),
                         rhs_scale=j_scales[:, m * P : (m + 1) * P],
                         start=True, stop=True,
                     )
-            nc.vector.tensor_copy(out=b_sb[:, gi, :, :, :], in_=bg_ps[:].rearrange("p h g c -> p c h g"))
+            return b_ps
+
+        def make_b_sb(m):
+            b_ps = tok_j_term(m)
+            nc.vector.tensor_copy(out=b_sb[:, POOL_M.index(m), :, :, :], in_=b_ps[:].rearrange("p h g c -> p c h g"))
 
         out_rows = out.rearrange("b (x n a) m e -> (b x) n a (m e)", x=2, n=N_BLOCKS, a=2)
 
@@ -193,63 +191,57 @@ def tile_simplemodel_pb_t_kernel(tc, tok, corr_w, corr_b, cross_w, cross_b, out)
         banks_of = {}
         rows_of = {}
 
-        def make_h(k):
-            a, n0, m = units[k]
+        def h_tile(k):
             p = group_of[k]
-            if k == first_of[p]:
+            if p not in grouped_of:
                 grouped_of[p] = g_pool.tile(
                     [P, GROUPS[p] * WINDOW, 2, 2], BF16, align_bytes=64, tag="g_grouped", name="g_grouped"
                 )
             first = (k - first_of[p]) * WINDOW
-            g_grouped = grouped_of[p][:, first : first + WINDOW, :, :]
+            return grouped_of[p][:, first : first + WINDOW, :, :]
+
+        def route(k):
+            return ROUTE[k] if len(ROUTE) == 32 else ROUTE[units[k][2]]
+
+        def pool_h(k):
+            a, n0, m = units[k]
+            stored = a_term[:, a, :, n0 * P : (n0 + 2) * P].rearrange("p h (l c) -> p l c h", l=2)
+            nc.gpsimd.tensor_tensor(
+                out=h_tile(k).rearrange("p (l c) h g -> p l c h g", l=2),
+                in0=b_sb[:, POOL_M.index(m), :, :, :].unsqueeze(1).to_broadcast([P, 2, P, 2, 2]),
+                in1=stored.unsqueeze(4).to_broadcast([P, 2, P, 2, 2]),
+                op=ADD,
+            )
+
+        def scalar_h(k):
+            a, n0, m = units[k]
             j_cols = slice(m * P, (m + 1) * P)
-            if ROUTE[m] == "G":
-                stored = a_term[:, a, :, n0 * P : (n0 + 2) * P].rearrange("p h (l c) -> p l c h", l=2)
-                nc.gpsimd.tensor_tensor(
-                    out=g_grouped.rearrange("p (l c) h g -> p l c h g", l=2),
-                    in0=b_sb[:, POOL_M.index(m), :, :, :].unsqueeze(1).to_broadcast([P, 2, P, 2, 2]),
-                    in1=stored.unsqueeze(4).to_broadcast([P, 2, P, 2, 2]),
-                    op=ADD,
-                )
-            elif ROUTE[m] == "V":
-                b_ps = psum_h.tile([P, 2, 2, P], F32, tag="h", name="b_ps")
-                for eh in range(2):
-                    for par in range(2):
-                        codes, scales = w1(1, par, eh)
-                        nc.tensor.matmul_mx(
-                            out=b_ps[:, eh, par, :], lhsT=codes, lhsT_scale=scales,
-                            rhs=j_codes[:, m * P : (m + 1) * P].bitcast(FP8X4),
-                            rhs_scale=j_scales[:, m * P : (m + 1) * P],
-                            start=True, stop=True,
-                        )
-                b_of[k] = b_ps
-            else:
-                for eh in range(2):
-                    h_ps = psum_h.tile([P, 2, WINDOW], F32, tag="h", name="h_ps")
-                    for par in range(2):
-                        codes, scales = w1(0, a, eh)
-                        nc.tensor.matmul_mx(
-                            out=h_ps[:, par, :], lhsT=codes, lhsT_scale=scales,
-                            rhs=i_codes[:, n0 * P : n0 * P + WINDOW].bitcast(FP8X4),
-                            rhs_scale=i_scales[:, n0 * P : n0 * P + WINDOW],
-                            start=True, stop=False,
-                        )
-                        codes, scales = w1(1, par, eh)
-                        for l in range(2):
-                            nc.tensor.matmul_mx(
-                                out=h_ps[:, par, l * P : (l + 1) * P], lhsT=codes, lhsT_scale=scales,
-                                rhs=j_codes[:, j_cols].bitcast(FP8X4), rhs_scale=j_scales[:, j_cols],
-                                start=False, stop=(l == 1),
-                            )
-                    nc.scalar.activation(
-                        out=g_grouped[:, :, eh, :], in_=h_ps[:].rearrange("p g c -> p c g"),
-                        func=IDENTITY, bias=corr_bias[:, eh : eh + 1], scale=1.0,
+            g_grouped = h_tile(k)
+            for eh in range(2):
+                h_ps = psum_h.tile([P, 2, WINDOW], F32, tag="h", name="h_ps")
+                for par in range(2):
+                    codes, scales = w1(0, a, eh)
+                    nc.tensor.matmul_mx(
+                        out=h_ps[:, par, :], lhsT=codes, lhsT_scale=scales,
+                        rhs=i_codes[:, n0 * P : n0 * P + WINDOW].bitcast(FP8X4),
+                        rhs_scale=i_scales[:, n0 * P : n0 * P + WINDOW],
+                        start=True, stop=False,
                     )
+                    codes, scales = w1(1, par, eh)
+                    for l in range(2):
+                        nc.tensor.matmul_mx(
+                            out=h_ps[:, par, l * P : (l + 1) * P], lhsT=codes, lhsT_scale=scales,
+                            rhs=j_codes[:, j_cols].bitcast(FP8X4), rhs_scale=j_scales[:, j_cols],
+                            start=False, stop=(l == 1),
+                        )
+                nc.scalar.activation(
+                    out=g_grouped[:, :, eh, :], in_=h_ps[:].rearrange("p g c -> p c g"),
+                    func=IDENTITY, bias=corr_bias[:, eh : eh + 1], scale=1.0,
+                )
 
         def vector_h(k):
             a, n0, m = units[k]
-            first = (k - first_of[group_of[k]]) * WINDOW
-            g_grouped = grouped_of[group_of[k]][:, first : first + WINDOW, :, :]
+            g_grouped = h_tile(k)
             for l in range(2):
                 n = n0 + l
                 stored = a_term[:, a, :, n * P : (n + 1) * P].rearrange("p h c -> p c h")
@@ -259,6 +251,14 @@ def tile_simplemodel_pb_t_kernel(tc, tok, corr_w, corr_b, cross_w, cross_b, out)
                     in1=stored.unsqueeze(3).to_broadcast([P, P, 2, 2]),
                     op=ADD,
                 )
+
+        def make_h(k):
+            if route(k) == "G":
+                pool_h(k)
+            elif route(k) == "V":
+                b_of[k] = tok_j_term(units[k][2])
+            else:
+                scalar_h(k)
 
         def quantise_g(k):
             codes = g_pool.tile([P, GROUPS[k] * WINDOW], U32, align_bytes=64, tag="g_codes", name="codes")
@@ -298,16 +298,40 @@ def tile_simplemodel_pb_t_kernel(tc, tok, corr_w, corr_b, cross_w, cross_b, out)
                     in_=rows[:].rearrange("p l m e -> p l (m e)"),
                 )
 
+        def cross_operands():
+            codes = const.tile([P, E], U32, align_bytes=64, name="w2_codes")
+            scales = const.tile([P, E], U8, align_bytes=64, name="w2_scales")
+            nc.vector.quantize_mx(
+                out=codes[:].bitcast(FP8X4), scales=scales[:], in_=w2_grouped[:].rearrange("p e t -> p (e t)")
+            )
+            bias = const.tile([P, E], F32, name="cross_bias")
+            nc.vector.tensor_copy(out=bias[:], in_=xb_ps[:])
+            return codes, scales, bias
+
+        w2_codes, w2_scales, cross_bias = cross_operands()
+
+        def before_step(step):
+            if step == 0:
+                make_a_term(0, 0, "V")
+                make_a_term(0, 1, "V")
+                make_b_sb(1)
+            if step == 3:
+                make_a_term(1, 0, "S")
+                move_windows(1, nc.vector)
+            if step == 4:
+                make_a_term(1, 1, "V")
+                make_b_sb(5)
+
         n_units = len(units)
-        with tc.manual_schedule():
-            for step in range(n_units + LAG_O):
-                if step - LAG_M in first_of:
-                    quantise_g(first_of.index(step - LAG_M))
-                if 0 <= step - LAG_O:
-                    bias_and_store(step - LAG_O)
-                if step < n_units:
-                    make_h(step)
-                if 0 <= step - LAG_V < n_units and ROUTE[units[step - LAG_V][2]] == "V":
-                    vector_h(step - LAG_V)
-                if 0 <= step - LAG_M < n_units:
-                    second_matmul(step - LAG_M)
+        for step in range(n_units + LAG_O):
+            before_step(step)
+            if step - LAG_M in first_of:
+                quantise_g(first_of.index(step - LAG_M))
+            if 0 <= step - LAG_O:
+                bias_and_store(step - LAG_O)
+            if step < n_units:
+                make_h(step)
+            if 0 <= step - LAG_V < n_units and route(step - LAG_V) == "V":
+                vector_h(step - LAG_V)
+            if 0 <= step - LAG_M < n_units:
+                second_matmul(step - LAG_M)

@@ -205,13 +205,15 @@ def tile_simplemodel_pb_t_kernel(tc, tok, corr_w, corr_b, cross_w, cross_b, out)
 
         def pool_h(k):
             a, n0, m = units[k]
-            stored = a_term[:, a, :, n0 * P : (n0 + 2) * P].rearrange("p h (l c) -> p l c h", l=2)
-            nc.gpsimd.tensor_tensor(
-                out=h_tile(k).rearrange("p (l c) h g -> p l c h g", l=2),
-                in0=b_sb[:, POOL_M.index(m), :, :, :].unsqueeze(1).to_broadcast([P, 2, P, 2, 2]),
-                in1=stored.unsqueeze(4).to_broadcast([P, 2, P, 2, 2]),
-                op=ADD,
-            )
+            g_grouped = h_tile(k)
+            for l in range(2):
+                stored = a_term[:, a, :, (n0 + l) * P : (n0 + l + 1) * P].rearrange("p h c -> p c h")
+                nc.gpsimd.tensor_tensor(
+                    out=g_grouped[:, l * P : (l + 1) * P, :, :],
+                    in0=b_sb[:, POOL_M.index(m), :, :, :],
+                    in1=stored.unsqueeze(3).to_broadcast([P, P, 2, 2]),
+                    op=ADD,
+                )
 
         def scalar_h(k):
             a, n0, m = units[k]

@@ -19,12 +19,14 @@ B, NTOK, E = 64, 16, 256
 M_OUT = NTOK // 2
 N_BLOCKS = 4
 WINDOW = 2 * P
+W_SCALES = P * PACK
+W_BYTES = W_SCALES + P
 M_PER_STORE = 2
-ROUTE = "VGSSSGSS"
+ROUTE = "VGSSSGVSSGSVSGSSSGSSVGSSSGSSSGSS"
 GROUPS = [4, 4, 4, 4, 4, 4, 4, 2, 1, 1]
-LAG_V = 1
-LAG_M = 8
-LAG_O = LAG_M + 2
+LAG_V = 2
+LAGS = [8] * 10
+LAG_O = 2
 
 FLOPS = 2 * B * NTOK * NTOK * 2 * E * E + 2 * B * NTOK * M_OUT * 2 * E * E
 
@@ -34,13 +36,14 @@ def tile_simplemodel_pb_t_kernel(tc, tok, corr_w, corr_b, cross_w, cross_b, out)
     with ExitStack() as ctx:
         const = ctx.enter_context(tc.tile_pool(name="const", bufs=1))
         g_pool = ctx.enter_context(tc.tile_pool(name="g", bufs=6))
-        out_pool = ctx.enter_context(tc.tile_pool(name="rows", bufs=4))
+        out_pool = ctx.enter_context(tc.tile_pool(name="rows", bufs=8))
         psum_h = ctx.enter_context(tc.psum_pool(name="psum_h", bufs=5))
         psum_o = ctx.enter_context(tc.psum_pool(name="psum_o", bufs=3))
         ctx.enter_context(tc.manual_schedule())
 
         cw_sb = const.tile([P, 2, 2 * E], BF16)
-        nc.sync.dma_start(out=cw_sb[:], in_=corr_w.rearrange("(h p) k -> p h k", p=P))
+        for eh in range(2):
+            nc.sync.dma_start(out=cw_sb[:, eh, :], in_=corr_w[eh * P : (eh + 1) * P, :])
         tok_sb = const.tile([P, 8 * E], BF16)
         tok_rows = tok.rearrange("b (x r) k -> (b x) (r k)", x=2)
         nc.sync.dma_start(out=tok_sb[:, 0 : 4 * E], in_=tok_rows[:, 0 : 4 * E])
@@ -58,14 +61,12 @@ def tile_simplemodel_pb_t_kernel(tc, tok, corr_w, corr_b, cross_w, cross_b, out)
         nc.sync.dma_start(out=xw_sb[:], in_=cross_w.rearrange("(h p) k -> p h k", p=P))
         ones = const.tile([P, P], BF16)
         nc.vector.memset(ones[:], 1.0)
-        w1_codes = const.tile([P, 4, 2 * P], U32, align_bytes=64)
-        w1_scales = const.tile([P, 4, 2 * P], U8, align_bytes=64)
-        nc.vector.memset(w1_codes[:].bitcast(I32), 0)
-        nc.vector.memset(w1_scales[:].bitcast(I32), 0)
-        i_scales = const.tile([P, N_BLOCKS * P], U8, align_bytes=64)
+        w1_all = const.tile([P, 4, 2, W_BYTES], U8, align_bytes=64)
+        nc.vector.memset(w1_all[:].bitcast(I32), 0)
+        i_scales = const.tile([P, 2, WINDOW], U8, align_bytes=64)
         nc.vector.memset(i_scales[:].bitcast(I32), 0)
-        w_scales = const.tile([P, 2 * P], U8, align_bytes=64)
-        nc.vector.memset(w_scales[:].bitcast(I32), 0)
+        w_all = const.tile([P, 2, W_BYTES], U8, align_bytes=64)
+        nc.vector.memset(w_all[:, :, W_SCALES:W_BYTES].bitcast(I32), 0)
         ident_bf = const.tile([P, P], BF16)
         nc.vector.tensor_copy(out=ident_bf[:], in_=ident_f32[:])
 
@@ -76,7 +77,12 @@ def tile_simplemodel_pb_t_kernel(tc, tok, corr_w, corr_b, cross_w, cross_b, out)
                 nc.tensor.transpose(wt[:, eh, u, :], cw_words[:, eh, u, :], ident_f32[:])
         w_grouped = const.tile([P, 2 * P * PACK], BF16, align_bytes=64)
         w_words = w_grouped[:].bitcast(F32).rearrange("p (h e u) -> p h e u", h=2, u=2)
-        nc.scalar.copy(out=w_words, in_=wt[:].rearrange("p h u e -> p h e u"))
+        for eh in range(2):
+            nc.scalar.copy(out=w_words[:, eh, :, :], in_=wt[:, eh, :, :].rearrange("p u e -> p e u"))
+            nc.vector.quantize_mx(
+                out=w_all[:, eh, 0:W_SCALES].bitcast(FP8X4), scales=w_all[:, eh, W_SCALES:W_BYTES],
+                in_=w_grouped[:, eh * P * PACK : (eh + 1) * P * PACK],
+            )
         tok_words = tok_sb[:].bitcast(F32).rearrange("p (n q u) -> p n u q", n=N_BLOCKS, u=2)
         i_grouped = const.tile([P, N_BLOCKS * P * PACK], BF16, align_bytes=64)
         i_words = i_grouped[:].bitcast(F32).rearrange("p (n c u) -> p n c u", n=N_BLOCKS, u=2)
@@ -87,22 +93,18 @@ def tile_simplemodel_pb_t_kernel(tc, tok, corr_w, corr_b, cross_w, cross_b, out)
                 for u in range(2):
                     nc.tensor.transpose(xt[:, nb, u, :], tok_words[:, 2 * pair + nb, u, :], ident_f32[:])
             xts.append(xt)
-        w_codes = const.tile([P, 2 * P], U32, align_bytes=64)
-        nc.vector.quantize_mx(out=w_codes[:].bitcast(FP8X4), scales=w_scales[:], in_=w_grouped[:])
-        for kind, half in ((0, 0), (1, 0), (1, 1), (0, 1)):
+        for eh, kind, half in ((0, 0, 0), (0, 1, 0), (0, 1, 1), (1, 0, 0), (1, 1, 0), (1, 1, 1), (0, 0, 1), (1, 0, 1)):
             rows = slice(HALF * half, HALF * (half + 1))
             source = slice(HALF * kind, HALF * (kind + 1))
             v = 2 * kind + half
-            nc.sync.dma_start(out=w1_codes[rows, v, :].bitcast(I32), in_=w_codes[source, :].bitcast(I32))
-            nc.sync.dma_start(out=w1_scales[rows, v, :].bitcast(I32), in_=w_scales[source, :].bitcast(I32))
+            nc.sync.dma_start(out=w1_all[rows, v, eh, :].bitcast(I32), in_=w_all[source, eh, :].bitcast(I32))
 
         def w1(kind, half, eh):
             v = 2 * kind + half
-            cols = slice(eh * P, (eh + 1) * P)
-            return w1_codes[:, v, cols].bitcast(FP8X4), w1_scales[:, v, cols]
+            return w1_all[:, v, eh, 0:W_SCALES].bitcast(FP8X4), w1_all[:, v, eh, W_SCALES:W_BYTES]
 
-        i_codes = const.tile([P, N_BLOCKS * P], U32, align_bytes=64)
-        for pair, copy in ((0, nc.scalar.copy), (1, nc.vector.tensor_copy)):
+        i_codes = const.tile([P, 2, WINDOW], U32, align_bytes=64)
+        for pair, copy in ((0, nc.scalar.copy), (1, nc.scalar.copy)):
             copy(out=i_words[:, 2 * pair : 2 * pair + 2, :, :], in_=xts[pair][:].rearrange("p n u c -> p n c u"))
         wct = psum_o.tile([P, PACK, E], BF16, tag="o")
         for eh in range(2):
@@ -119,25 +121,30 @@ def tile_simplemodel_pb_t_kernel(tc, tok, corr_w, corr_b, cross_w, cross_b, out)
         w2_grouped = const.tile([P, E, PACK], BF16, align_bytes=64)
         nc.scalar.copy(out=w2_grouped[:], in_=wct[:].rearrange("p t e -> p e t"))
 
-        nc.vector.quantize_mx(out=i_codes[:].bitcast(FP8X4), scales=i_scales[:], in_=i_grouped[:])
         corr_bias = const.tile([P, 2], F32)
-        nc.vector.tensor_copy(out=corr_bias[:], in_=cbt[:, 0:2])
 
         j_codes = const.tile([P, M_OUT * P], U32, align_bytes=64)
         j_scales = const.tile([P, M_OUT * P], U8, align_bytes=64)
-        i_code_cols = i_codes[:].bitcast(I32).rearrange("p (n b x) -> p x n b", n=N_BLOCKS, x=2)
-        j_code_cols = j_codes[:].bitcast(I32).rearrange("p (x n b d) -> p x n b d", x=2, n=N_BLOCKS, d=2)
-        i_scale_cols = i_scales[:].rearrange("p (n b x) -> p x n b", n=N_BLOCKS, x=2)
-        j_scale_cols = j_scales[:].rearrange("p (x n b d) -> p x d n b", x=2, n=N_BLOCKS, d=2)
+        i_code_cols = i_codes[:].bitcast(I32).rearrange("p q (n b x) -> p x q n b", n=2, x=2)
+        j_code_cols = j_codes[:].bitcast(I32).rearrange("p (x q n b d) -> p x q n b d", x=2, q=2, n=2, d=2)
+        i_scale_cols = i_scales[:].rearrange("p q (n b x) -> p x q n b", n=2, x=2)
+        j_scale_cols = j_scales[:].rearrange("p (x q n b d) -> p x d q n b", x=2, q=2, n=2, d=2)
 
-        def move_windows(x, engine):
-            engine.tensor_copy(
-                out=j_code_cols[:, x, :, :, :], in_=i_code_cols[:, x, :, :].unsqueeze(3).to_broadcast([P, N_BLOCKS, B, 2])
+        def move_windows(x, q):
+            nc.vector.tensor_copy(
+                out=j_code_cols[:, x, q], in_=i_code_cols[:, x, q].unsqueeze(3).to_broadcast([P, 2, B, 2])
             )
             for d in range(2):
-                engine.tensor_copy(out=j_scale_cols[:, x, d, :, :], in_=i_scale_cols[:, x, :, :])
+                nc.vector.tensor_copy(out=j_scale_cols[:, x, d, q], in_=i_scale_cols[:, x, q])
 
-        move_windows(0, nc.vector)
+        for q in range(2):
+            nc.vector.quantize_mx(
+                out=i_codes[:, q, :].bitcast(FP8X4), scales=i_scales[:, q, :],
+                in_=i_grouped[:, q * WINDOW * PACK : (q + 1) * WINDOW * PACK],
+            )
+            if q == 0:
+                nc.vector.tensor_copy(out=corr_bias[:], in_=cbt[:, 0:2])
+            move_windows(0, q)
 
         a_term = const.tile([P, 2, 2, N_BLOCKS * P], F32)
 
@@ -145,7 +152,8 @@ def tile_simplemodel_pb_t_kernel(tc, tok, corr_w, corr_b, cross_w, cross_b, out)
             a_ps = psum_h.tile([P, N_BLOCKS * P], F32, tag="h", name="a_ps")
             codes, scales = w1(0, a, eh)
             nc.tensor.matmul_mx(
-                out=a_ps[:], lhsT=codes, lhsT_scale=scales, rhs=i_codes[:].bitcast(FP8X4), rhs_scale=i_scales[:],
+                out=a_ps[:], lhsT=codes, lhsT_scale=scales, rhs=i_codes[:].rearrange("p q c -> p (q c)").bitcast(FP8X4),
+                rhs_scale=i_scales[:].rearrange("p q c -> p (q c)"),
                 start=True, stop=True,
             )
             if engine == "S":
@@ -173,9 +181,10 @@ def tile_simplemodel_pb_t_kernel(tc, tok, corr_w, corr_b, cross_w, cross_b, out)
                     )
             return b_ps
 
-        def make_b_sb(m):
+        def make_b_sb(m, engine="V"):
             b_ps = tok_j_term(m)
-            nc.vector.tensor_copy(out=b_sb[:, POOL_M.index(m), :, :, :], in_=b_ps[:].rearrange("p h g c -> p c h g"))
+            copy = nc.scalar.copy if engine == "S" else nc.vector.tensor_copy
+            copy(out=b_sb[:, POOL_M.index(m), :, :, :], in_=b_ps[:].rearrange("p h g c -> p c h g"))
 
         out_rows = out.rearrange("b (x n a) m e -> (b x) n a (m e)", x=2, n=N_BLOCKS, a=2)
 
@@ -225,8 +234,7 @@ def tile_simplemodel_pb_t_kernel(tc, tok, corr_w, corr_b, cross_w, cross_b, out)
                     codes, scales = w1(0, a, eh)
                     nc.tensor.matmul_mx(
                         out=h_ps[:, par, :], lhsT=codes, lhsT_scale=scales,
-                        rhs=i_codes[:, n0 * P : n0 * P + WINDOW].bitcast(FP8X4),
-                        rhs_scale=i_scales[:, n0 * P : n0 * P + WINDOW],
+                        rhs=i_codes[:, n0 // 2, :].bitcast(FP8X4), rhs_scale=i_scales[:, n0 // 2, :],
                         start=True, stop=False,
                     )
                     codes, scales = w1(1, par, eh)
@@ -272,6 +280,7 @@ def tile_simplemodel_pb_t_kernel(tc, tok, corr_w, corr_b, cross_w, cross_b, out)
 
         def second_matmul(k):
             codes, scales = codes_of[group_of[k]]
+            w2_codes, w2_scales, cross_bias = w2
             first = (k - first_of[group_of[k]]) * WINDOW
             o_ps = psum_o.tile([P, 2, E], F32, tag="o", name="o_ps")
             for l in range(2):
@@ -289,6 +298,7 @@ def tile_simplemodel_pb_t_kernel(tc, tok, corr_w, corr_b, cross_w, cross_b, out)
             if m % M_PER_STORE == 0:
                 rows_of[0] = out_pool.tile([P, 2, M_PER_STORE, E], F32, tag="rows", name="rows")
             rows = rows_of[0]
+            cross_bias = w2[2]
             nc.vector.tensor_tensor(
                 out=rows[:, :, m % M_PER_STORE, :], in0=banks_of[k][:],
                 in1=cross_bias[:].unsqueeze(1).to_broadcast([P, 2, E]), op=ADD,
@@ -310,30 +320,43 @@ def tile_simplemodel_pb_t_kernel(tc, tok, corr_w, corr_b, cross_w, cross_b, out)
             nc.vector.tensor_copy(out=bias[:], in_=xb_ps[:])
             return codes, scales, bias
 
-        w2_codes, w2_scales, cross_bias = cross_operands()
+        w2 = []
+
+        START = {0: ["X", "A00V", "B1S", "A01V", "A10S", "A11V"], 3: ["W"], 4: ["B5V"]}
 
         def before_step(step):
-            if step == 0:
-                make_a_term(0, 0, "V")
-                make_a_term(0, 1, "V")
-                make_b_sb(1)
-            if step == 3:
-                make_a_term(1, 0, "S")
-                move_windows(1, nc.vector)
-            if step == 4:
-                make_a_term(1, 1, "V")
-                make_b_sb(5)
+            for t in START.get(step, []):
+                if t[0] == "A":
+                    make_a_term(int(t[1]), int(t[2]), t[3])
+                elif t[0] == "B":
+                    make_b_sb(int(t[1]), t[2])
+                elif t[0] == "X":
+                    move_windows(1, 0)
+                    move_windows(1, 1)
+                elif t[0] == "W":
+                    w2.extend(cross_operands())
+                elif t[0] == "V":
+                    vector_h(int(t[1:]))
 
         n_units = len(units)
-        for step in range(n_units + LAG_O):
+        quantise_at = {}
+        multiply_at = {}
+        store_at = {}
+        for k in range(n_units):
+            p = group_of[k]
+            if k == first_of[p]:
+                quantise_at.setdefault(k + LAGS[p], []).append(p)
+            multiply_at.setdefault(k + LAGS[p], []).append(k)
+            store_at.setdefault(k + LAGS[p] + LAG_O, []).append(k)
+        for step in range(max(store_at) + 1):
             before_step(step)
-            if step - LAG_M in first_of:
-                quantise_g(first_of.index(step - LAG_M))
-            if 0 <= step - LAG_O:
-                bias_and_store(step - LAG_O)
+            for p in quantise_at.get(step, []):
+                quantise_g(p)
+            for k in store_at.get(step, []):
+                bias_and_store(k)
             if step < n_units:
                 make_h(step)
             if 0 <= step - LAG_V < n_units and route(step - LAG_V) == "V":
                 vector_h(step - LAG_V)
-            if 0 <= step - LAG_M < n_units:
-                second_matmul(step - LAG_M)
+            for k in multiply_at.get(step, []):
+                second_matmul(k)

@@ -22,8 +22,9 @@ WINDOW = 2 * P
 W_SCALES = P * PACK
 W_BYTES = W_SCALES + P
 M_PER_STORE = 2
-ROUTE = "VGSSSGVSSGSVSGSSSGSSVGSSSGSSSGSS"
+ROUTE = "VGSVSGSVSGSVSGSSSGSSVGSSSGSSSGSS"
 GROUPS = [4, 4, 4, 4, 4, 4, 4, 2, 1, 1]
+ALONE = 30
 LAG_V = 2
 LAGS = [8] * 10
 LAG_O = 2
@@ -53,14 +54,10 @@ def tile_simplemodel_pb_t_kernel(tc, tok, corr_w, corr_b, cross_w, cross_b, out)
         nc.scalar.activation(out=warm[:, 1:2], in_=warm[:, 0:1], func=IDENTITY, scale=1.0)
         ident_f32 = const.tile([P, P], F32)
         make_identity(nc, ident_f32[:])
-        bias_rows = const.tile([P, P + E], BF16)
-        nc.vector.memset(bias_rows[:], 0.0)
-        nc.sync.dma_start(out=bias_rows[0:2, 0:P], in_=corr_b.rearrange("(h e) -> h e", h=2))
-        nc.sync.dma_start(out=bias_rows[0:1, P : P + E], in_=cross_b.rearrange("(o e) -> o e", o=1))
+        corr_bias = const.tile([P, 2], BF16)
+        nc.sync.dma_start(out=corr_bias[:], in_=corr_b.rearrange("(h p) -> p h", h=2))
         xw_sb = const.tile([P, 2, 2 * E], BF16)
         nc.sync.dma_start(out=xw_sb[:], in_=cross_w.rearrange("(h p) k -> p h k", p=P))
-        ones = const.tile([P, P], BF16)
-        nc.vector.memset(ones[:], 1.0)
         w1_all = const.tile([P, 4, 2, W_BYTES], U8, align_bytes=64)
         nc.vector.memset(w1_all[:].bitcast(I32), 0)
         i_scales = const.tile([P, 2, WINDOW], U8, align_bytes=64)
@@ -99,6 +96,9 @@ def tile_simplemodel_pb_t_kernel(tc, tok, corr_w, corr_b, cross_w, cross_b, out)
             v = 2 * kind + half
             nc.sync.dma_start(out=w1_all[rows, v, eh, :].bitcast(I32), in_=w_all[source, eh, :].bitcast(I32))
 
+        cross_bias = const.tile([P, E], BF16)
+        nc.sync.dma_start(out=cross_bias[:], in_=cross_b.partition_broadcast(P))
+
         def w1(kind, half, eh):
             v = 2 * kind + half
             return w1_all[:, v, eh, 0:W_SCALES].bitcast(FP8X4), w1_all[:, v, eh, W_SCALES:W_BYTES]
@@ -114,14 +114,9 @@ def tile_simplemodel_pb_t_kernel(tc, tok, corr_w, corr_b, cross_w, cross_b, out)
                     nc.tensor.transpose(
                         wct[:, 2 * eh + par, hh * P : (hh + 1) * P], xw_sb[:, hh, first : first + P], ident_bf[:]
                     )
-        cbt = psum_o.tile([P, P], BF16, tag="o")
-        nc.tensor.transpose(cbt[:], bias_rows[:, 0:P], ident_bf[:])
-        xb_ps = psum_o.tile([P, E], F32, tag="o")
-        nc.tensor.matmul(out=xb_ps[:], lhsT=ones[:], rhs=bias_rows[:, P : P + E], start=True, stop=True)
         w2_grouped = const.tile([P, E, PACK], BF16, align_bytes=64)
         nc.scalar.copy(out=w2_grouped[:], in_=wct[:].rearrange("p t e -> p e t"))
 
-        corr_bias = const.tile([P, 2], F32)
 
         j_codes = const.tile([P, M_OUT * P], U32, align_bytes=64)
         j_scales = const.tile([P, M_OUT * P], U8, align_bytes=64)
@@ -130,21 +125,19 @@ def tile_simplemodel_pb_t_kernel(tc, tok, corr_w, corr_b, cross_w, cross_b, out)
         i_scale_cols = i_scales[:].rearrange("p q (n b x) -> p x q n b", n=2, x=2)
         j_scale_cols = j_scales[:].rearrange("p (x q n b d) -> p x d q n b", x=2, q=2, n=2, d=2)
 
-        def move_windows(x, q):
+        def move_windows(q):
             nc.vector.tensor_copy(
-                out=j_code_cols[:, x, q], in_=i_code_cols[:, x, q].unsqueeze(3).to_broadcast([P, 2, B, 2])
+                out=j_code_cols[:, :, q], in_=i_code_cols[:, :, q].unsqueeze(4).to_broadcast([P, 2, 2, B, 2])
             )
             for d in range(2):
-                nc.vector.tensor_copy(out=j_scale_cols[:, x, d, q], in_=i_scale_cols[:, x, q])
+                nc.vector.tensor_copy(out=j_scale_cols[:, :, d, q], in_=i_scale_cols[:, :, q])
 
         for q in range(2):
             nc.vector.quantize_mx(
                 out=i_codes[:, q, :].bitcast(FP8X4), scales=i_scales[:, q, :],
                 in_=i_grouped[:, q * WINDOW * PACK : (q + 1) * WINDOW * PACK],
             )
-            if q == 0:
-                nc.vector.tensor_copy(out=corr_bias[:], in_=cbt[:, 0:2])
-            move_windows(0, q)
+            move_windows(q)
 
         a_term = const.tile([P, 2, 2, N_BLOCKS * P], F32)
 
@@ -280,7 +273,7 @@ def tile_simplemodel_pb_t_kernel(tc, tok, corr_w, corr_b, cross_w, cross_b, out)
 
         def second_matmul(k):
             codes, scales = codes_of[group_of[k]]
-            w2_codes, w2_scales, cross_bias = w2
+            w2_codes, w2_scales = w2[0], w2[1]
             first = (k - first_of[group_of[k]]) * WINDOW
             o_ps = psum_o.tile([P, 2, E], F32, tag="o", name="o_ps")
             for l in range(2):
@@ -298,12 +291,13 @@ def tile_simplemodel_pb_t_kernel(tc, tok, corr_w, corr_b, cross_w, cross_b, out)
             if m % M_PER_STORE == 0:
                 rows_of[0] = out_pool.tile([P, 2, M_PER_STORE, E], F32, tag="rows", name="rows")
             rows = rows_of[0]
-            cross_bias = w2[2]
-            nc.vector.tensor_tensor(
-                out=rows[:, :, m % M_PER_STORE, :], in0=banks_of[k][:],
-                in1=cross_bias[:].unsqueeze(1).to_broadcast([P, 2, E]), op=ADD,
-            )
-            if m % M_PER_STORE == M_PER_STORE - 1:
+            bias = cross_bias[:].unsqueeze(1).to_broadcast([P, 2, E])
+            nc.vector.tensor_tensor(out=rows[:, :, m % M_PER_STORE, :], in0=banks_of[k][:], in1=bias, op=ADD)
+            if k >= ALONE:
+                nc.sync.dma_start(
+                    out=out_rows[:, n0 : n0 + 2, a, m * E : (m + 1) * E], in_=rows[:, :, m % M_PER_STORE, :],
+                )
+            elif m % M_PER_STORE == M_PER_STORE - 1:
                 first = (m + 1 - M_PER_STORE) * E
                 nc.sync.dma_start(
                     out=out_rows[:, n0 : n0 + 2, a, first : first + M_PER_STORE * E],
@@ -316,13 +310,11 @@ def tile_simplemodel_pb_t_kernel(tc, tok, corr_w, corr_b, cross_w, cross_b, out)
             nc.vector.quantize_mx(
                 out=codes[:].bitcast(FP8X4), scales=scales[:], in_=w2_grouped[:].rearrange("p e t -> p (e t)")
             )
-            bias = const.tile([P, E], F32, name="cross_bias")
-            nc.vector.tensor_copy(out=bias[:], in_=xb_ps[:])
-            return codes, scales, bias
+            return codes, scales, cross_bias
 
         w2 = []
 
-        START = {0: ["X", "A00V", "B1S", "A01V", "A10S", "A11V"], 3: ["W"], 4: ["B5V"]}
+        START = {0: ["A00S", "B1V", "A01S", "A10V", "A11S"], 3: ["W"], 4: ["B5S"]}
 
         def before_step(step):
             for t in START.get(step, []):
@@ -331,8 +323,7 @@ def tile_simplemodel_pb_t_kernel(tc, tok, corr_w, corr_b, cross_w, cross_b, out)
                 elif t[0] == "B":
                     make_b_sb(int(t[1]), t[2])
                 elif t[0] == "X":
-                    move_windows(1, 0)
-                    move_windows(1, 1)
+                    pass
                 elif t[0] == "W":
                     w2.extend(cross_operands())
                 elif t[0] == "V":

@@ -97,7 +97,6 @@ def tile_simplemodel_pb_t_kernel(tc, tok, corr_w, corr_b, cross_w, cross_b, out)
             nc.sync.dma_start(out=w1_all[rows, v, eh, :].bitcast(I32), in_=w_all[source, eh, :].bitcast(I32))
 
         cross_bias = const.tile([P, E], BF16)
-        nc.sync.dma_start(out=cross_bias[:], in_=cross_b.partition_broadcast(P))
 
         def w1(kind, half, eh):
             v = 2 * kind + half
@@ -314,7 +313,7 @@ def tile_simplemodel_pb_t_kernel(tc, tok, corr_w, corr_b, cross_w, cross_b, out)
 
         w2 = []
 
-        START = {0: ["A00S", "B1V", "A01S", "A10V", "A11S"], 3: ["W"], 4: ["B5S"]}
+        START = {0: ["A00S", "B1V", "A01S", "A10V", "A11S"], 3: ["W", "C"], 4: ["B5S"]}
 
         def before_step(step):
             for t in START.get(step, []):
@@ -322,8 +321,8 @@ def tile_simplemodel_pb_t_kernel(tc, tok, corr_w, corr_b, cross_w, cross_b, out)
                     make_a_term(int(t[1]), int(t[2]), t[3])
                 elif t[0] == "B":
                     make_b_sb(int(t[1]), t[2])
-                elif t[0] == "X":
-                    pass
+                elif t[0] == "C":
+                    nc.scalar.dma_start(out=cross_bias[:], in_=cross_b.partition_broadcast(P))
                 elif t[0] == "W":
                     w2.extend(cross_operands())
                 elif t[0] == "V":

@@ -52,6 +52,15 @@ def tile_simplemodel_pb_t_kernel(tc, tok, corr_w, corr_b, cross_w, cross_b, out)
         warm = const.tile([P, 2], F32)
         nc.vector.memset(warm[:], 0.0)
         nc.scalar.activation(out=warm[:, 1:2], in_=warm[:, 0:1], func=IDENTITY, scale=1.0)
+        idle = const.tile([P, 4 * P], BF16)
+        nc.vector.memset(idle[:], 0.0)
+
+        def keep_busy(count):
+            bank = psum_o.tile([P, 4 * P], F32, tag="o", name="idle_ps")
+            for i in range(count):
+                nc.tensor.matmul(out=bank[:], lhsT=idle[:, 0:P], rhs=idle[:], start=True, stop=True)
+
+        keep_busy(4)
         ident_f32 = const.tile([P, P], F32)
         make_identity(nc, ident_f32[:])
         corr_bias = const.tile([P, 2], BF16)
@@ -80,6 +89,7 @@ def tile_simplemodel_pb_t_kernel(tc, tok, corr_w, corr_b, cross_w, cross_b, out)
                 out=w_all[:, eh, 0:W_SCALES].bitcast(FP8X4), scales=w_all[:, eh, W_SCALES:W_BYTES],
                 in_=w_grouped[:, eh * P * PACK : (eh + 1) * P * PACK],
             )
+        keep_busy(1)
         tok_words = tok_sb[:].bitcast(F32).rearrange("p (n q u) -> p n u q", n=N_BLOCKS, u=2)
         i_grouped = const.tile([P, N_BLOCKS * P * PACK], BF16, align_bytes=64)
         i_words = i_grouped[:].bitcast(F32).rearrange("p (n c u) -> p n c u", n=N_BLOCKS, u=2)
@@ -90,6 +100,7 @@ def tile_simplemodel_pb_t_kernel(tc, tok, corr_w, corr_b, cross_w, cross_b, out)
                 for u in range(2):
                     nc.tensor.transpose(xt[:, nb, u, :], tok_words[:, 2 * pair + nb, u, :], ident_f32[:])
             xts.append(xt)
+        keep_busy(1)
         for eh, kind, half in ((0, 0, 0), (0, 1, 0), (0, 1, 1), (1, 0, 0), (1, 1, 0), (1, 1, 1), (0, 0, 1), (1, 0, 1)):
             rows = slice(HALF * half, HALF * (half + 1))
             source = slice(HALF * kind, HALF * (kind + 1))
@@ -113,6 +124,7 @@ def tile_simplemodel_pb_t_kernel(tc, tok, corr_w, corr_b, cross_w, cross_b, out)
                     nc.tensor.transpose(
                         wct[:, 2 * eh + par, hh * P : (hh + 1) * P], xw_sb[:, hh, first : first + P], ident_bf[:]
                     )
+        keep_busy(3)
         w2_grouped = const.tile([P, E, PACK], BF16, align_bytes=64)
         nc.scalar.copy(out=w2_grouped[:], in_=wct[:].rearrange("p t e -> p e t"))
 

from contextlib import ExitStack

import concourse.mybir as mybir
from concourse.masks import make_identity

F32 = mybir.dt.float32
BF16 = mybir.dt.bfloat16
U32 = mybir.dt.uint32
U8 = mybir.dt.uint8
I32 = mybir.dt.int32
FP8X4 = mybir.dt.float8_e4m3fn_x4
ADD = mybir.AluOpType.add
IDENTITY = mybir.ActivationFunctionType.Identity

P = 128
PACK = 4
HALF = 64
B, NTOK, E = 64, 16, 256
M_OUT = NTOK // 2
N_BLOCKS = 4
WINDOW = 2 * P
W_SCALES = P * PACK
W_BYTES = W_SCALES + P
M_PER_STORE = 2
ROUTE = "VGSVSGSVSGSVSGSSSGSSVGSSSGSSSGSS"
GROUPS = [4, 4, 4, 4, 4, 4, 4, 2, 1, 1]
ALONE = 30
LAG_V = 2
LAGS = [8] * 10
LAG_O = 2

FLOPS = 2 * B * NTOK * NTOK * 2 * E * E + 2 * B * NTOK * M_OUT * 2 * E * E


def tile_simplemodel_pb_t_kernel(tc, tok, corr_w, corr_b, cross_w, cross_b, out):
    nc = tc.nc
    with ExitStack() as ctx:
        const = ctx.enter_context(tc.tile_pool(name="const", bufs=1))
        g_pool = ctx.enter_context(tc.tile_pool(name="g", bufs=6))
        out_pool = ctx.enter_context(tc.tile_pool(name="rows", bufs=8))
        psum_h = ctx.enter_context(tc.psum_pool(name="psum_h", bufs=5))
        psum_o = ctx.enter_context(tc.psum_pool(name="psum_o", bufs=3))
        ctx.enter_context(tc.manual_schedule())

        cw_sb = const.tile([P, 2, 2 * E], BF16)
        for eh in range(2):
            nc.sync.dma_start(out=cw_sb[:, eh, :], in_=corr_w[eh * P : (eh + 1) * P, :])
        tok_sb = const.tile([P, 8 * E], BF16)
        tok_rows = tok.rearrange("b (x r) k -> (b x) (r k)", x=2)
        nc.sync.dma_start(out=tok_sb[:, 0 : 4 * E], in_=tok_rows[:, 0 : 4 * E])
        nc.sync.dma_start(out=tok_sb[:, 4 * E : 8 * E], in_=tok_rows[:, 4 * E : 8 * E])
        warm = const.tile([P, 2], F32)
        nc.vector.memset(warm[:], 0.0)
        nc.scalar.activation(out=warm[:, 1:2], in_=warm[:, 0:1], func=IDENTITY, scale=1.0)
        idle = const.tile([P, 4 * P], BF16)
        nc.vector.memset(idle[:], 0.0)

        def keep_busy(count):
            bank = psum_o.tile([P, 4 * P], F32, tag="o", name="idle_ps")
            for i in range(count):
                nc.tensor.matmul(out=bank[:], lhsT=idle[:, 0:P], rhs=idle[:], start=True, stop=True)

        keep_busy(4)
        ident_f32 = const.tile([P, P], F32)
        make_identity(nc, ident_f32[:])
        corr_bias = const.tile([P, 2], BF16)
        nc.sync.dma_start(out=corr_bias[:], in_=corr_b.rearrange("(h p) -> p h", h=2))
        xw_sb = const.tile([P, 2, 2 * E], BF16)
        nc.sync.dma_start(out=xw_sb[:], in_=cross_w.rearrange("(h p) k -> p h k", p=P))
        w1_all = const.tile([P, 4, 2, W_BYTES], U8, align_bytes=64)
        nc.vector.memset(w1_all[:].bitcast(I32), 0)
        i_scales = const.tile([P, 2, WINDOW], U8, align_bytes=64)
        nc.vector.memset(i_scales[:].bitcast(I32), 0)
        w_all = const.tile([P, 2, W_BYTES], U8, align_bytes=64)
        nc.vector.memset(w_all[:, :, W_SCALES:W_BYTES].bitcast(I32), 0)
        ident_bf = const.tile([P, P], BF16)
        nc.vector.tensor_copy(out=ident_bf[:], in_=ident_f32[:])

        cw_words = cw_sb[:].rearrange("p h k -> p (h k)").bitcast(F32).rearrange("p (h q u) -> p h u q", h=2, u=2)
        wt = psum_h.tile([P, 2, 2, P], F32, tag="h", name="wt")
        for eh in range(2):
            for u in range(2):
                nc.tensor.transpose(wt[:, eh, u, :], cw_words[:, eh, u, :], ident_f32[:])
        w_grouped = const.tile([P, 2 * P * PACK], BF16, align_bytes=64)
        w_words = w_grouped[:].bitcast(F32).rearrange("p (h e u) -> p h e u", h=2, u=2)
        for eh in range(2):
            nc.scalar.copy(out=w_words[:, eh, :, :], in_=wt[:, eh, :, :].rearrange("p u e -> p e u"))
            nc.vector.quantize_mx(
                out=w_all[:, eh, 0:W_SCALES].bitcast(FP8X4), scales=w_all[:, eh, W_SCALES:W_BYTES],
                in_=w_grouped[:, eh * P * PACK : (eh + 1) * P * PACK],
            )
        keep_busy(1)
        tok_words = tok_sb[:].bitcast(F32).rearrange("p (n q u) -> p n u q", n=N_BLOCKS, u=2)
        i_grouped = const.tile([P, N_BLOCKS * P * PACK], BF16, align_bytes=64)
        i_words = i_grouped[:].bitcast(F32).rearrange("p (n c u) -> p n c u", n=N_BLOCKS, u=2)
        xts = []
        for pair in range(2):
            xt = psum_h.tile([P, 2, 2, P], F32, tag="h", name="xt%d" % pair)
            for nb in range(2):
                for u in range(2):
                    nc.tensor.transpose(xt[:, nb, u, :], tok_words[:, 2 * pair + nb, u, :], ident_f32[:])
            xts.append(xt)
        keep_busy(1)
        for eh, kind, half in ((0, 0, 0), (0, 1, 0), (0, 1, 1), (1, 0, 0), (1, 1, 0), (1, 1, 1), (0, 0, 1), (1, 0, 1)):
            rows = slice(HALF * half, HALF * (half + 1))
            source = slice(HALF * kind, HALF * (kind + 1))
            v = 2 * kind + half
            nc.sync.dma_start(out=w1_all[rows, v, eh, :].bitcast(I32), in_=w_all[source, eh, :].bitcast(I32))

        cross_bias = const.tile([P, E], BF16)

        def w1(kind, half, eh):
            v = 2 * kind + half
            return w1_all[:, v, eh, 0:W_SCALES].bitcast(FP8X4), w1_all[:, v, eh, W_SCALES:W_BYTES]

        i_codes = const.tile([P, 2, WINDOW], U32, align_bytes=64)
        for pair, copy in ((0, nc.scalar.copy), (1, nc.scalar.copy)):
            copy(out=i_words[:, 2 * pair : 2 * pair + 2, :, :], in_=xts[pair][:].rearrange("p n u c -> p n c u"))
        wct = psum_o.tile([P, PACK, E], BF16, tag="o")
        for eh in range(2):
            for par in range(2):
                for hh in range(2):
                    first = E * par + P * eh
                    nc.tensor.transpose(
                        wct[:, 2 * eh + par, hh * P : (hh + 1) * P], xw_sb[:, hh, first : first + P], ident_bf[:]
                    )
        keep_busy(3)
        w2_grouped = const.tile([P, E, PACK], BF16, align_bytes=64)
        nc.scalar.copy(out=w2_grouped[:], in_=wct[:].rearrange("p t e -> p e t"))


        j_codes = const.tile([P, M_OUT * P], U32, align_bytes=64)
        j_scales = const.tile([P, M_OUT * P], U8, align_bytes=64)
        i_code_cols = i_codes[:].bitcast(I32).rearrange("p q (n b x) -> p x q n b", n=2, x=2)
        j_code_cols = j_codes[:].bitcast(I32).rearrange("p (x q n b d) -> p x q n b d", x=2, q=2, n=2, d=2)
        i_scale_cols = i_scales[:].rearrange("p q (n b x) -> p x q n b", n=2, x=2)
        j_scale_cols = j_scales[:].rearrange("p (x q n b d) -> p x d q n b", x=2, q=2, n=2, d=2)

        def move_windows(q):
            nc.vector.tensor_copy(
                out=j_code_cols[:, :, q], in_=i_code_cols[:, :, q].unsqueeze(4).to_broadcast([P, 2, 2, B, 2])
            )
            for d in range(2):
                nc.vector.tensor_copy(out=j_scale_cols[:, :, d, q], in_=i_scale_cols[:, :, q])

        for q in range(2):
            nc.vector.quantize_mx(
                out=i_codes[:, q, :].bitcast(FP8X4), scales=i_scales[:, q, :],
                in_=i_grouped[:, q * WINDOW * PACK : (q + 1) * WINDOW * PACK],
            )
            move_windows(q)

        a_term = const.tile([P, 2, 2, N_BLOCKS * P], F32)

        def make_a_term(a, eh, engine):
            a_ps = psum_h.tile([P, N_BLOCKS * P], F32, tag="h", name="a_ps")
            codes, scales = w1(0, a, eh)
            nc.tensor.matmul_mx(
                out=a_ps[:], lhsT=codes, lhsT_scale=scales, rhs=i_codes[:].rearrange("p q c -> p (q c)").bitcast(FP8X4),
                rhs_scale=i_scales[:].rearrange("p q c -> p (q c)"),
                start=True, stop=True,
            )
            if engine == "S":
                nc.scalar.activation(
                    out=a_term[:, a, eh, :], in_=a_ps[:], func=IDENTITY, bias=corr_bias[:, eh : eh + 1], scale=1.0
                )
            else:
                nc.vector.tensor_scalar(
                    out=a_term[:, a, eh, :], in0=a_ps[:], scalar1=corr_bias[:, eh : eh + 1], scalar2=None, op0=ADD
                )

        POOL_M = [1, 5]
        b_sb = const.tile([P, len(POOL_M), P, 2, 2], F32)

        def tok_j_term(m):
            b_ps = psum_h.tile([P, 2, 2, P], F32, tag="h", name="b_ps")
            for eh in range(2):
                for par in range(2):
                    codes, scales = w1(1, par, eh)
                    nc.tensor.matmul_mx(
                        out=b_ps[:, eh, par, :], lhsT=codes, lhsT_scale=scales,
                        rhs=j_codes[:, m * P : (m + 1) * P].bitcast(FP8X4),
                        rhs_scale=j_scales[:, m * P : (m + 1) * P],
                        start=True, stop=True,
                    )
            return b_ps

        def make_b_sb(m, engine="V"):
            b_ps = tok_j_term(m)
            copy = nc.scalar.copy if engine == "S" else nc.vector.tensor_copy
            copy(out=b_sb[:, POOL_M.index(m), :, :, :], in_=b_ps[:].rearrange("p h g c -> p c h g"))

        out_rows = out.rearrange("b (x n a) m e -> (b x) n a (m e)", x=2, n=N_BLOCKS, a=2)

        units = [(a, n0, m) for a in range(2) for n0 in range(0, N_BLOCKS, 2) for m in range(M_OUT)]
        group_of = []
        first_of = []
        for p, size in enumerate(GROUPS):
            first_of.append(len(group_of))
            group_of.extend([p] * size)
        grouped_of = {}
        b_of = {}
        codes_of = {}
        banks_of = {}
        rows_of = {}

        def h_tile(k):
            p = group_of[k]
            if p not in grouped_of:
                grouped_of[p] = g_pool.tile(
                    [P, GROUPS[p] * WINDOW, 2, 2], BF16, align_bytes=64, tag="g_grouped", name="g_grouped"
                )
            first = (k - first_of[p]) * WINDOW
            return grouped_of[p][:, first : first + WINDOW, :, :]

        def route(k):
            return ROUTE[k] if len(ROUTE) == 32 else ROUTE[units[k][2]]

        def pool_h(k):
            a, n0, m = units[k]
            g_grouped = h_tile(k)
            for l in range(2):
                stored = a_term[:, a, :, (n0 + l) * P : (n0 + l + 1) * P].rearrange("p h c -> p c h")
                nc.gpsimd.tensor_tensor(
                    out=g_grouped[:, l * P : (l + 1) * P, :, :],
                    in0=b_sb[:, POOL_M.index(m), :, :, :],
                    in1=stored.unsqueeze(3).to_broadcast([P, P, 2, 2]),
                    op=ADD,
                )

        def scalar_h(k):
            a, n0, m = units[k]
            j_cols = slice(m * P, (m + 1) * P)
            g_grouped = h_tile(k)
            for eh in range(2):
                h_ps = psum_h.tile([P, 2, WINDOW], F32, tag="h", name="h_ps")
                for par in range(2):
                    codes, scales = w1(0, a, eh)
                    nc.tensor.matmul_mx(
                        out=h_ps[:, par, :], lhsT=codes, lhsT_scale=scales,
                        rhs=i_codes[:, n0 // 2, :].bitcast(FP8X4), rhs_scale=i_scales[:, n0 // 2, :],
                        start=True, stop=False,
                    )
                    codes, scales = w1(1, par, eh)
                    for l in range(2):
                        nc.tensor.matmul_mx(
                            out=h_ps[:, par, l * P : (l + 1) * P], lhsT=codes, lhsT_scale=scales,
                            rhs=j_codes[:, j_cols].bitcast(FP8X4), rhs_scale=j_scales[:, j_cols],
                            start=False, stop=(l == 1),
                        )
                nc.scalar.activation(
                    out=g_grouped[:, :, eh, :], in_=h_ps[:].rearrange("p g c -> p c g"),
                    func=IDENTITY, bias=corr_bias[:, eh : eh + 1], scale=1.0,
                )

        def vector_h(k):
            a, n0, m = units[k]
            g_grouped = h_tile(k)
            for l in range(2):
                n = n0 + l
                stored = a_term[:, a, :, n * P : (n + 1) * P].rearrange("p h c -> p c h")
                nc.vector.tensor_tensor(
                    out=g_grouped[:, l * P : (l + 1) * P, :, :],
                    in0=b_of[k][:].rearrange("p h g c -> p c h g"),
                    in1=stored.unsqueeze(3).to_broadcast([P, P, 2, 2]),
                    op=ADD,
                )

        def make_h(k):
            if route(k) == "G":
                pool_h(k)
            elif route(k) == "V":
                b_of[k] = tok_j_term(units[k][2])
            else:
                scalar_h(k)

        def quantise_g(k):
            codes = g_pool.tile([P, GROUPS[k] * WINDOW], U32, align_bytes=64, tag="g_codes", name="codes")
            scales = g_pool.tile([P, GROUPS[k] * WINDOW], U8, align_bytes=64, tag="g_scales", name="scales")
            nc.vector.quantize_mx(
                out=codes[:].bitcast(FP8X4), scales=scales[:], in_=grouped_of[k][:].rearrange("p c h g -> p (c h g)")
            )
            codes_of[k] = (codes, scales)

        def second_matmul(k):
            codes, scales = codes_of[group_of[k]]
            w2_codes, w2_scales = w2[0], w2[1]
            first = (k - first_of[group_of[k]]) * WINDOW
            o_ps = psum_o.tile([P, 2, E], F32, tag="o", name="o_ps")
            for l in range(2):
                cols = slice(first + l * P, first + (l + 1) * P)
                nc.tensor.matmul_mx(
                    out=o_ps[:, l, :],
                    lhsT=codes[:, cols].bitcast(FP8X4), lhsT_scale=scales[:, cols],
                    rhs=w2_codes[:].bitcast(FP8X4), rhs_scale=w2_scales[:],
                    start=True, stop=True,
                )
            banks_of[k] = o_ps

        def bias_and_store(k):
            a, n0, m = units[k]
            if m % M_PER_STORE == 0:
                rows_of[0] = out_pool.tile([P, 2, M_PER_STORE, E], F32, tag="rows", name="rows")
            rows = rows_of[0]
            bias = cross_bias[:].unsqueeze(1).to_broadcast([P, 2, E])
            nc.vector.tensor_tensor(out=rows[:, :, m % M_PER_STORE, :], in0=banks_of[k][:], in1=bias, op=ADD)
            if k >= ALONE:
                nc.sync.dma_start(
                    out=out_rows[:, n0 : n0 + 2, a, m * E : (m + 1) * E], in_=rows[:, :, m % M_PER_STORE, :],
                )
            elif m % M_PER_STORE == M_PER_STORE - 1:
                first = (m + 1 - M_PER_STORE) * E
                nc.sync.dma_start(
                    out=out_rows[:, n0 : n0 + 2, a, first : first + M_PER_STORE * E],
                    in_=rows[:].rearrange("p l m e -> p l (m e)"),
                )

        def cross_operands():
            codes = const.tile([P, E], U32, align_bytes=64, name="w2_codes")
            scales = const.tile([P, E], U8, align_bytes=64, name="w2_scales")
            nc.vector.quantize_mx(
                out=codes[:].bitcast(FP8X4), scales=scales[:], in_=w2_grouped[:].rearrange("p e t -> p (e t)")
            )
            return codes, scales, cross_bias

        w2 = []

        START = {0: ["A00S", "B1V", "A01S", "A10V", "A11S"], 3: ["W", "C"], 4: ["B5S"]}

        def before_step(step):
            for t in START.get(step, []):
                if t[0] == "A":
                    make_a_term(int(t[1]), int(t[2]), t[3])
                elif t[0] == "B":
                    make_b_sb(int(t[1]), t[2])
                elif t[0] == "C":
                    nc.scalar.dma_start(out=cross_bias[:], in_=cross_b.partition_broadcast(P))
                elif t[0] == "W":
                    w2.extend(cross_operands())
                elif t[0] == "V":
                    vector_h(int(t[1:]))

        n_units = len(units)
        quantise_at = {}
        multiply_at = {}
        store_at = {}
        for k in range(n_units):
            p = group_of[k]
            if k == first_of[p]:
                quantise_at.setdefault(k + LAGS[p], []).append(p)
            multiply_at.setdefault(k + LAGS[p], []).append(k)
            store_at.setdefault(k + LAGS[p] + LAG_O, []).append(k)
        for step in range(max(store_at) + 1):
            before_step(step)
            for p in quantise_at.get(step, []):
                quantise_g(p)
            for k in store_at.get(step, []):
                bias_and_store(k)
            if step < n_units:
                make_h(step)
            if 0 <= step - LAG_V < n_units and route(step - LAG_V) == "V":
                vector_h(step - LAG_V)
            for k in multiply_at.get(step, []):
                second_matmul(k)
